import numpy as np
import ml_dtypes


def mxq(x, axis, fmt="e4m3"):
    dtype, down = {"e4m3": (ml_dtypes.float8_e4m3fn, 7), "e5m2": (ml_dtypes.float8_e5m2, 14)}[fmt]
    v = np.moveaxis(np.asarray(x, np.float32).astype(ml_dtypes.bfloat16).astype(np.float64), axis, -1)
    blocks = v.reshape(v.shape[:-1] + (-1, 32))
    amax = np.abs(blocks).max(-1, keepdims=True)
    byte = np.maximum(np.where(amax > 0, np.frexp(amax)[1] - 1 + 127, 0) - down, 1)
    scale = np.exp2(byte - 127.0)
    codes = (blocks / scale).astype(np.float32).astype(dtype).astype(np.float64)
    return np.moveaxis((codes * scale).reshape(v.shape), -1, axis)


WIDE = False


def mx_kscale(k):
    if not WIDE:
        return np.ones(k)
    levels = np.array([10, -10, 5, -5, 0])
    a = np.random.permutation(np.resize(levels, k // 512 * 4)).reshape(k // 512, 4)
    idx = np.arange(k)
    return np.exp2(a[idx // 512, idx % 128 // 32])


BF16 = ml_dtypes.bfloat16


def bf(x):
    return np.asarray(x, np.float32).astype(BF16)


def f64(x):
    return np.asarray(x).astype(np.float64)


N, T, V, K, CB, S, CIN = 2, 4, 128, 4, 512, 4, 4096
EPS = 1e-5
KV = K * V


def setup_inputs():
    s = mx_kscale(CB)
    u = mx_kscale(KV)[::V]
    ur = np.repeat(u, CB)
    return {"sp_prev": bf(np.maximum(np.random.standard_normal((N, CB, T, V)), 0.0) * s[None, :, None, None]),
            "spx": bf(np.maximum(np.random.standard_normal((N, CB, T, V)), 0.0) * 1.1 * s[None, :, None, None]),
            "gcn_w": bf(np.random.standard_normal((K * CB, CB)) * 0.8 / np.sqrt(CB) / s[None, :] * ur[:, None]),
            "gcn_b": bf(np.random.standard_normal(K * CB) * 0.3 * ur),
            "A": bf((np.random.uniform(size=(K, V, V)) - 0.5) * 3.0 / np.sqrt(KV) / u[:, None, None]),
            "PA": bf(np.random.standard_normal((K, V, V)) * 0.4 / np.sqrt(KV) / u[:, None, None]),
            "bg": bf(np.random.uniform(size=CB) + 0.5),
            "bb": bf(np.random.standard_normal(CB) * 0.2),
            "bm": bf(np.random.standard_normal(CB) * 0.2),
            "bv": bf(np.random.uniform(size=CB) + 0.5)}


def reference(sp_prev, spx, gcn_w, gcn_b, A, PA, bg, bb, bm, bv):
    sp = f64(sp_prev) + f64(spx)
    g = (mxq(np.moveaxis(sp, 1, 3), 3, "e4m3") @ mxq(f64(gcn_w), 1, "e4m3").T) + f64(gcn_b)
    g = np.swapaxes(np.moveaxis(g.reshape(N, T, V, K, CB), -1, 1), 3, -1).reshape(N, CB, T, KV)
    adj = (f64(A) + f64(PA)).reshape(KV, V)
    y = mxq(g, 3, "e4m3") @ mxq(adj, 0, "e4m3")
    scale = f64(bg) / np.sqrt(f64(bv) + EPS)
    shift = f64(bb) - f64(bm) * scale
    return np.maximum(y * scale[None, :, None, None] + shift[None, :, None, None], 0.0)

@@ -1,0 +1,212 @@
+from contextlib import ExitStack
+
+import concourse.mybir as mybir
+from concourse.masks import make_identity
+
+BF16 = mybir.dt.bfloat16
+F32 = mybir.dt.float32
+I32 = mybir.dt.int32
+U32 = mybir.dt.uint32
+U8 = mybir.dt.uint8
+FP8X4 = mybir.dt.float8_e4m3fn_x4
+ADD = mybir.AluOpType.add
+RELU = mybir.ActivationFunctionType.Relu
+
+P = 128
+PACK = 4
+BATCH, FRAMES, JOINTS, SUBSETS, CHANNELS = 2, 4, 128, 4, 512
+CHUNKS = CHANNELS // P
+TOKENS = FRAMES * JOINTS
+WIDE = P * SUBSETS
+EPS = 1e-5
+
+FLOPS = 2 * BATCH * TOKENS * SUBSETS * CHANNELS * CHANNELS + 2 * BATCH * FRAMES * CHANNELS * SUBSETS * JOINTS * JOINTS
+
+
+def tile_ms_spatial_bottleneck_layer_pa_kernel(tc, sp_prev, spx, gcn_w, gcn_b, A, PA, bg, bb, bm, bv, out):
+    nc = tc.nc
+    with ExitStack() as stack:
+        keep = stack.enter_context(tc.tile_pool(name="keep", bufs=1))
+        work = stack.enter_context(tc.tile_pool(name="work", bufs=3))
+        acc_psum = stack.enter_context(tc.psum_pool(name="acc_psum", bufs=4))
+        turn_psum = stack.enter_context(tc.psum_pool(name="turn_psum", bufs=2))
+        y_psum = stack.enter_context(tc.psum_pool(name="y_psum", bufs=2))
+
+        ident_f32 = keep.tile([P, P], F32)
+        make_identity(nc, ident_f32[:])
+
+        bias_row = keep.tile([P, SUBSETS * CHANNELS], BF16)
+        nc.vector.memset(bias_row[:].bitcast(I32), 0)
+        nc.sync.dma_start(out=bias_row[0:1, :], in_=gcn_b.unsqueeze(0))
+        ones = keep.tile([P, P], BF16)
+        nc.vector.memset(ones[:], 1.0)
+        a_raw = keep.tile([P, SUBSETS, JOINTS], BF16)
+        pa_raw = keep.tile([P, SUBSETS, JOINTS], BF16)
+        nc.sync.dma_start(out=a_raw[:], in_=A.rearrange("k v w -> v k w"))
+        nc.sync.dma_start(out=pa_raw[:], in_=PA.rearrange("k v w -> v k w"))
+
+        prev_raw = keep.tile([P, BATCH, PACK, TOKENS], BF16)
+        x_raw = keep.tile([P, BATCH, PACK, TOKENS], BF16)
+        w_raw = keep.tile([P, CHUNKS, SUBSETS, CHANNELS], BF16)
+        w_rows = gcn_w.rearrange("(k cc p) c -> cc p k c", k=SUBSETS, cc=CHUNKS)
+
+        def load_activations(n):
+            for raw, src in ((prev_raw, sp_prev), (x_raw, spx)):
+                nc.sync.dma_start(
+                    out=raw[:, n].rearrange("q (u e) x -> q u (e x)", u=2),
+                    in_=src[n].rearrange("(u q e) t v -> q u (e t v)", u=2, e=2),
+                )
+
+        load_activations(0)
+        nc.sync.dma_start(out=w_raw[:, 0], in_=w_rows[0])
+        load_activations(1)
+        for cc in range(1, CHUNKS):
+            nc.sync.dma_start(out=w_raw[:, cc], in_=w_rows[cc])
+
+        bn_rows = keep.tile([P, P], BF16)
+        nc.vector.memset(bn_rows[:], 0.0)
+        for i, vec in enumerate((bg, bb, bm, bv)):
+            nc.gpsimd.dma_start(out=bn_rows[CHUNKS * i : CHUNKS * (i + 1), :], in_=vec.rearrange("(cc p) -> cc p", p=P))
+
+        bias_all = keep.tile([P, SUBSETS * CHANNELS], BF16)
+        for k in range(SUBSETS):
+            spread = acc_psum.tile([P, CHANNELS], F32, tag="acc")
+            nc.tensor.matmul(spread[:], lhsT=ones[:], rhs=bias_row[:, k * CHANNELS : (k + 1) * CHANNELS], start=True, stop=True)
+            nc.scalar.copy(out=bias_all[:, k * CHANNELS : (k + 1) * CHANNELS], in_=spread[:])
+        bias_by_chunk = bias_all[:].rearrange("p (k cc c) -> p cc c k", k=SUBSETS, cc=CHUNKS)
+
+        adj_sum = keep.tile([P, SUBSETS, JOINTS], BF16)
+        nc.vector.tensor_tensor(out=adj_sum[:], in0=a_raw[:], in1=pa_raw[:], op=ADD)
+        adj_grouped = keep.tile([P, JOINTS, SUBSETS], BF16, align_bytes=64)
+        nc.vector.tensor_copy(out=adj_grouped[:], in_=adj_sum[:].rearrange("v k w -> v w k"))
+        adj_codes = keep.tile([P, JOINTS], U32, align_bytes=64)
+        adj_scales = keep.tile([P, JOINTS], U8, align_bytes=64)
+        nc.vector.quantize_mx(
+            out=adj_codes[:].bitcast(FP8X4), scales=adj_scales[:], in_=adj_grouped[:].rearrange("v w k -> v (w k)")
+        )
+
+        sp_sum = keep.tile([P, BATCH, PACK, TOKENS], BF16)
+        sp_grouped = keep.tile([P, BATCH, TOKENS, PACK], BF16, align_bytes=64)
+        sp_codes = keep.tile([P, BATCH, TOKENS], U32, align_bytes=64)
+        sp_scales = keep.tile([P, BATCH, TOKENS], U8, align_bytes=64)
+
+        def prepare_activations(n, copy):
+            nc.vector.tensor_tensor(out=sp_sum[:, n], in0=prev_raw[:, n], in1=x_raw[:, n], op=ADD)
+            copy(
+                out=sp_grouped[:, n].rearrange("q (x i) j -> q x j i", i=4),
+                in_=sp_sum[:, n].rearrange("q j (x i) -> q x j i", i=4),
+            )
+            nc.vector.quantize_mx(
+                out=sp_codes[:, n].bitcast(FP8X4), scales=sp_scales[:, n], in_=sp_grouped[:, n].rearrange("q x j -> q (x j)")
+            )
+
+        w_grouped = keep.tile([P, CHUNKS, WIDE * PACK], BF16, align_bytes=64)
+        w_codes = keep.tile([P, CHUNKS, WIDE], U32, align_bytes=64)
+        w_scales = keep.tile([P, CHUNKS, WIDE], U8, align_bytes=64)
+
+        def prepare_weights(cc):
+            words_out = w_grouped[:, cc].bitcast(F32).rearrange("q (c k u) -> q c k u", k=SUBSETS, u=2)
+            for pair in range(SUBSETS // 2):
+                turned = turn_psum.tile([P, 2, 2, P], F32, tag="turn")
+                for k2 in range(2):
+                    for u in range(2):
+                        nc.tensor.transpose(
+                            turned[:, k2, u, :], w_raw[:, cc, 2 * pair + k2, :].bitcast(F32)[:, u * P : (u + 1) * P], ident_f32[:]
+                        )
+                nc.scalar.copy(out=words_out[:, :, 2 * pair : 2 * pair + 2, :], in_=turned[:].rearrange("q k u c -> q c k u"))
+            nc.vector.quantize_mx(out=w_codes[:, cc].bitcast(FP8X4), scales=w_scales[:, cc], in_=w_grouped[:, cc])
+
+        def prepare_batch_norm():
+            ident_bf16 = keep.tile([P, P], BF16)
+            nc.vector.tensor_copy(out=ident_bf16[:], in_=ident_f32[:])
+            bn_turned = turn_psum.tile([P, P], BF16, tag="turn")
+            nc.tensor.transpose(bn_turned[:], bn_rows[:], ident_bf16[:])
+            bn_cols = keep.tile([P, 4, CHUNKS], F32)
+            nc.vector.tensor_copy(out=bn_cols[:], in_=bn_turned[:, 0 : 4 * CHUNKS].rearrange("p (i cc) -> p i cc", i=4))
+            var_eps = keep.tile([P, CHUNKS], F32)
+            nc.vector.tensor_scalar_add(out=var_eps[:], in0=bn_cols[:, 3], scalar1=EPS)
+            std = keep.tile([P, CHUNKS], F32)
+            nc.scalar.sqrt(out=std[:], in_=var_eps[:])
+            inv_std = keep.tile([P, CHUNKS], F32)
+            nc.vector.reciprocal(out=inv_std[:], in_=std[:])
+            bn_scale = keep.tile([P, CHUNKS], F32)
+            nc.vector.tensor_mul(out=bn_scale[:], in0=bn_cols[:, 0], in1=inv_std[:])
+            mean_scaled = keep.tile([P, CHUNKS], F32)
+            nc.vector.tensor_mul(out=mean_scaled[:], in0=bn_cols[:, 2], in1=bn_scale[:])
+            bn_shift = keep.tile([P, CHUNKS], F32)
+            nc.vector.tensor_sub(out=bn_shift[:], in0=bn_cols[:, 1], in1=mean_scaled[:])
+            return bn_scale, bn_shift
+
+        def first_passes(n, cc):
+            banks = []
+            for t in range(FRAMES):
+                joints = slice(t * JOINTS, (t + 1) * JOINTS)
+                acc = acc_psum.tile([P, WIDE], F32, tag="acc")
+                nc.tensor.matmul_mx(
+                    out=acc[:],
+                    lhsT=sp_codes[:, n, joints].bitcast(FP8X4),
+                    lhsT_scale=sp_scales[:, n, joints],
+                    rhs=w_codes[:, cc].bitcast(FP8X4),
+                    rhs_scale=w_scales[:, cc],
+                    start=True,
+                    stop=True,
+                )
+                banks.append(acc)
+            return banks
+
+        def add_bias(acc, cc, g_frame):
+            nc.vector.tensor_tensor(
+                out=g_frame.rearrange("v (c k) -> v c k", k=SUBSETS),
+                in0=acc[:].rearrange("v (c k) -> v c k", k=SUBSETS),
+                in1=bias_by_chunk[:, cc],
+                op=ADD,
+            )
+
+        def second_layer(n, cc, g_grouped):
+            g_codes = work.tile([P, FRAMES, P], U32, align_bytes=64)
+            g_scales = work.tile([P, FRAMES, P], U8, align_bytes=64)
+            nc.vector.quantize_mx(
+                out=g_codes[:].rearrange("v t c -> v (t c)").bitcast(FP8X4),
+                scales=g_scales[:].rearrange("v t c -> v (t c)"),
+                in_=g_grouped[:].rearrange("v t x -> v (t x)"),
+            )
+            y = y_psum.tile([P, FRAMES, JOINTS], F32)
+            for t in range(FRAMES):
+                nc.tensor.matmul_mx(
+                    out=y[:, t],
+                    lhsT=g_codes[:, t].bitcast(FP8X4),
+                    lhsT_scale=g_scales[:, t],
+                    rhs=adj_codes[:].bitcast(FP8X4),
+                    rhs_scale=adj_scales[:],
+                    start=True,
+                    stop=True,
+                )
+            result = work.tile([P, FRAMES * JOINTS], F32)
+            nc.scalar.activation(
+                out=result[:],
+                in_=y[:].rearrange("c t w -> c (t w)"),
+                func=RELU,
+                bias=bn_shift[:, cc : cc + 1],
+                scale=bn_scale[:, cc : cc + 1],
+            )
+            nc.sync.dma_start(out=out[n, cc * P : (cc + 1) * P].rearrange("c t w -> c (t w)"), in_=result[:])
+
+        prepare_activations(0, nc.vector.tensor_copy)
+        prepare_weights(0)
+        prepare_activations(1, nc.scalar.copy)
+        bn_scale, bn_shift = prepare_batch_norm()
+
+        late = None
+        for cc in range(CHUNKS):
+            for n in range(BATCH):
+                banks = first_passes(n, cc)
+                g_grouped = work.tile([P, FRAMES, WIDE], BF16, align_bytes=64)
+                add_bias(banks[0], cc, g_grouped[:, 0])
+                if late is not None:
+                    second_layer(*late)
+                late = (n, cc, g_grouped)
+                if n == 0 and cc + 1 < CHUNKS:
+                    prepare_weights(cc + 1)
+                for t in range(1, FRAMES):
+                    add_bias(banks[t], cc, g_grouped[:, t])
+        second_layer(*late)

@@ -68,12 +68,13 @@ def tile_ms_spatial_bottleneck_layer_pa_kernel(tc, sp_prev, spx, gcn_w, gcn_b, A
         for i, vec in enumerate((bg, bb, bm, bv)):
             nc.gpsimd.dma_start(out=bn_rows[CHUNKS * i : CHUNKS * (i + 1), :], in_=vec.rearrange("(cc p) -> cc p", p=P))
 
-        bias_all = keep.tile([P, SUBSETS * CHANNELS], BF16)
-        for k in range(SUBSETS):
-            spread = acc_psum.tile([P, CHANNELS], F32, tag="acc")
-            nc.tensor.matmul(spread[:], lhsT=ones[:], rhs=bias_row[:, k * CHANNELS : (k + 1) * CHANNELS], start=True, stop=True)
-            nc.scalar.copy(out=bias_all[:, k * CHANNELS : (k + 1) * CHANNELS], in_=spread[:])
-        bias_by_chunk = bias_all[:].rearrange("p (k cc c) -> p cc c k", k=SUBSETS, cc=CHUNKS)
+        bias_all = keep.tile([P, CHUNKS, WIDE], BF16)
+        for cc in range(CHUNKS):
+            spread = acc_psum.tile([P, P, SUBSETS], F32, tag="acc")
+            for k in range(SUBSETS):
+                first = k * CHANNELS + cc * P
+                nc.tensor.matmul(spread[:, :, k], lhsT=ones[:], rhs=bias_row[:, first : first + P], start=True, stop=True)
+            nc.scalar.copy(out=bias_all[:, cc], in_=spread[:].rearrange("p c k -> p (c k)"))
 
         adj_sum = keep.tile([P, SUBSETS, JOINTS], BF16)
         nc.vector.tensor_tensor(out=adj_sum[:], in0=a_raw[:], in1=pa_raw[:], op=ADD)
@@ -155,12 +156,7 @@ def tile_ms_spatial_bottleneck_layer_pa_kernel(tc, sp_prev, spx, gcn_w, gcn_b, A
             return banks
 
         def add_bias(acc, cc, g_frame):
-            nc.vector.tensor_tensor(
-                out=g_frame.rearrange("v (c k) -> v c k", k=SUBSETS),
-                in0=acc[:].rearrange("v (c k) -> v c k", k=SUBSETS),
-                in1=bias_by_chunk[:, cc],
-                op=ADD,
-            )
+            nc.vector.tensor_tensor(out=g_frame, in0=acc[:], in1=bias_all[:, cc], op=ADD)
 
         def second_layer(n, cc, g_grouped):
             g_codes = work.tile([P, FRAMES, P], U32, align_bytes=64)

@@ -11,6 +11,7 @@ U8 = mybir.dt.uint8
 FP8X4 = mybir.dt.float8_e4m3fn_x4
 ADD = mybir.AluOpType.add
 RELU = mybir.ActivationFunctionType.Relu
+SQRT = mybir.ActivationFunctionType.Sqrt
 
 P = 128
 PACK = 4
@@ -18,6 +19,7 @@ BATCH, FRAMES, JOINTS, SUBSETS, CHANNELS = 2, 4, 128, 4, 512
 CHUNKS = CHANNELS // P
 TOKENS = FRAMES * JOINTS
 WIDE = P * SUBSETS
+ROUNDS = BATCH * CHUNKS
 EPS = 1e-5
 
 FLOPS = 2 * BATCH * TOKENS * SUBSETS * CHANNELS * CHANNELS + 2 * BATCH * FRAMES * CHANNELS * SUBSETS * JOINTS * JOINTS
@@ -27,85 +29,85 @@ def tile_ms_spatial_bottleneck_layer_pa_kernel(tc, sp_prev, spx, gcn_w, gcn_b, A
     nc = tc.nc
     with ExitStack() as stack:
         keep = stack.enter_context(tc.tile_pool(name="keep", bufs=1))
-        work = stack.enter_context(tc.tile_pool(name="work", bufs=3))
-        acc_psum = stack.enter_context(tc.psum_pool(name="acc_psum", bufs=4))
+        work = stack.enter_context(tc.tile_pool(name="work", bufs=2))
+        acc_psum = stack.enter_context(tc.psum_pool(name="acc_psum", bufs=FRAMES - 1))
+        side_psum = stack.enter_context(tc.psum_pool(name="side_psum", bufs=1))
         turn_psum = stack.enter_context(tc.psum_pool(name="turn_psum", bufs=2))
         y_psum = stack.enter_context(tc.psum_pool(name="y_psum", bufs=2))
+        stack.enter_context(tc.manual_schedule())
 
+        bn_rows = keep.tile([P, P], BF16)
+        nc.vector.memset(bn_rows[:], 0.0)
+        ones = keep.tile([P, P], BF16)
+        nc.vector.memset(ones[:], 1.0)
+        eps = keep.tile([P, 1], F32)
+        nc.vector.memset(eps[:], EPS)
+        warm = keep.tile([P, 1], F32)
+        nc.scalar.sqrt(out=warm[:], in_=eps[:])
+        for i, vec in enumerate((bg, bb, bm, bv)):
+            nc.gpsimd.dma_start(out=bn_rows[CHUNKS * i : CHUNKS * (i + 1), :], in_=vec.rearrange("(cc p) -> cc p", p=P))
         ident_f32 = keep.tile([P, P], F32)
         make_identity(nc, ident_f32[:])
 
         bias_row = keep.tile([P, SUBSETS * CHANNELS], BF16)
         nc.vector.memset(bias_row[:].bitcast(I32), 0)
-        nc.sync.dma_start(out=bias_row[0:1, :], in_=gcn_b.unsqueeze(0))
-        ones = keep.tile([P, P], BF16)
-        nc.vector.memset(ones[:], 1.0)
-        a_raw = keep.tile([P, SUBSETS, JOINTS], BF16)
-        pa_raw = keep.tile([P, SUBSETS, JOINTS], BF16)
-        nc.sync.dma_start(out=a_raw[:], in_=A.rearrange("k v w -> v k w"))
-        nc.sync.dma_start(out=pa_raw[:], in_=PA.rearrange("k v w -> v k w"))
-
         prev_raw = keep.tile([P, BATCH, PACK, TOKENS], BF16)
         x_raw = keep.tile([P, BATCH, PACK, TOKENS], BF16)
-        w_raw = keep.tile([P, CHUNKS, SUBSETS, CHANNELS], BF16)
-        w_rows = gcn_w.rearrange("(k cc p) c -> cc p k c", k=SUBSETS, cc=CHUNKS)
-
-        def load_activations(n):
+        for n in range(BATCH):
             for raw, src in ((prev_raw, sp_prev), (x_raw, spx)):
                 nc.sync.dma_start(
                     out=raw[:, n].rearrange("q (u e) x -> q u (e x)", u=2),
                     in_=src[n].rearrange("(u q e) t v -> q u (e t v)", u=2, e=2),
                 )
-
-        load_activations(0)
-        nc.sync.dma_start(out=w_raw[:, 0], in_=w_rows[0])
-        load_activations(1)
-        for cc in range(1, CHUNKS):
+        nc.sync.dma_start(out=bias_row[0:1, :], in_=gcn_b.unsqueeze(0))
+        a_raw = keep.tile([P, SUBSETS, JOINTS], BF16)
+        pa_raw = keep.tile([P, SUBSETS, JOINTS], BF16)
+        nc.sync.dma_start(out=a_raw[:], in_=A.rearrange("k v w -> v k w"))
+        nc.sync.dma_start(out=pa_raw[:], in_=PA.rearrange("k v w -> v k w"))
+        w_raw = keep.tile([P, CHUNKS, SUBSETS, CHANNELS], BF16)
+        w_rows = gcn_w.rearrange("(k cc p) c -> cc p k c", k=SUBSETS, cc=CHUNKS)
+        for cc in range(CHUNKS):
             nc.sync.dma_start(out=w_raw[:, cc], in_=w_rows[cc])
-
-        bn_rows = keep.tile([P, P], BF16)
-        nc.vector.memset(bn_rows[:], 0.0)
-        for i, vec in enumerate((bg, bb, bm, bv)):
-            nc.gpsimd.dma_start(out=bn_rows[CHUNKS * i : CHUNKS * (i + 1), :], in_=vec.rearrange("(cc p) -> cc p", p=P))
 
         bias_all = keep.tile([P, CHUNKS, WIDE], BF16)
         for cc in range(CHUNKS):
-            spread = acc_psum.tile([P, P, SUBSETS], F32, tag="acc")
+            spread = turn_psum.tile([P, P, SUBSETS], F32, tag="turn")
             for k in range(SUBSETS):
                 first = k * CHANNELS + cc * P
                 nc.tensor.matmul(spread[:, :, k], lhsT=ones[:], rhs=bias_row[:, first : first + P], start=True, stop=True)
             nc.scalar.copy(out=bias_all[:, cc], in_=spread[:].rearrange("p c k -> p (c k)"))
 
+        sp_sum = keep.tile([P, BATCH, PACK, TOKENS], BF16)
+        sp_grouped = keep.tile([P, BATCH, TOKENS, PACK], BF16, align_bytes=64)
+        sp_codes = keep.tile([P, BATCH, TOKENS], U32, align_bytes=64)
+        sp_scales = keep.tile([P, BATCH, TOKENS], U8, align_bytes=64)
+        for n in range(BATCH):
+            nc.vector.tensor_tensor(out=sp_sum[:, n], in0=prev_raw[:, n], in1=x_raw[:, n], op=ADD)
+            nc.vector.tensor_copy(
+                out=sp_grouped[:, n].rearrange("q (x i) j -> q x j i", i=4),
+                in_=sp_sum[:, n].rearrange("q j (x i) -> q x j i", i=4),
+            )
+        for n in range(BATCH):
+            nc.vector.quantize_mx(
+                out=sp_codes[:, n].bitcast(FP8X4), scales=sp_scales[:, n], in_=sp_grouped[:, n].rearrange("q x j -> q (x j)")
+            )
+
         adj_sum = keep.tile([P, SUBSETS, JOINTS], BF16)
         nc.vector.tensor_tensor(out=adj_sum[:], in0=a_raw[:], in1=pa_raw[:], op=ADD)
         adj_grouped = keep.tile([P, JOINTS, SUBSETS], BF16, align_bytes=64)
         nc.vector.tensor_copy(out=adj_grouped[:], in_=adj_sum[:].rearrange("v k w -> v w k"))
+        ident_bf16 = keep.tile([P, P], BF16)
+        nc.vector.tensor_copy(out=ident_bf16[:], in_=ident_f32[:])
         adj_codes = keep.tile([P, JOINTS], U32, align_bytes=64)
         adj_scales = keep.tile([P, JOINTS], U8, align_bytes=64)
         nc.vector.quantize_mx(
             out=adj_codes[:].bitcast(FP8X4), scales=adj_scales[:], in_=adj_grouped[:].rearrange("v w k -> v (w k)")
         )
 
-        sp_sum = keep.tile([P, BATCH, PACK, TOKENS], BF16)
-        sp_grouped = keep.tile([P, BATCH, TOKENS, PACK], BF16, align_bytes=64)
-        sp_codes = keep.tile([P, BATCH, TOKENS], U32, align_bytes=64)
-        sp_scales = keep.tile([P, BATCH, TOKENS], U8, align_bytes=64)
-
-        def prepare_activations(n, copy):
-            nc.vector.tensor_tensor(out=sp_sum[:, n], in0=prev_raw[:, n], in1=x_raw[:, n], op=ADD)
-            copy(
-                out=sp_grouped[:, n].rearrange("q (x i) j -> q x j i", i=4),
-                in_=sp_sum[:, n].rearrange("q j (x i) -> q x j i", i=4),
-            )
-            nc.vector.quantize_mx(
-                out=sp_codes[:, n].bitcast(FP8X4), scales=sp_scales[:, n], in_=sp_grouped[:, n].rearrange("q x j -> q (x j)")
-            )
-
         w_grouped = keep.tile([P, CHUNKS, WIDE * PACK], BF16, align_bytes=64)
         w_codes = keep.tile([P, CHUNKS, WIDE], U32, align_bytes=64)
         w_scales = keep.tile([P, CHUNKS, WIDE], U8, align_bytes=64)
-
-        def prepare_weights(cc):
+        for cc in range(CHUNKS):
             words_out = w_grouped[:, cc].bitcast(F32).rearrange("q (c k u) -> q c k u", k=SUBSETS, u=2)
             for pair in range(SUBSETS // 2):
                 turned = turn_psum.tile([P, 2, 2, P], F32, tag="turn")
@@ -117,57 +119,73 @@ def tile_ms_spatial_bottleneck_layer_pa_kernel(tc, sp_prev, spx, gcn_w, gcn_b, A
                 nc.scalar.copy(out=words_out[:, :, 2 * pair : 2 * pair + 2, :], in_=turned[:].rearrange("q k u c -> q c k u"))
             nc.vector.quantize_mx(out=w_codes[:, cc].bitcast(FP8X4), scales=w_scales[:, cc], in_=w_grouped[:, cc])
 
-        def prepare_batch_norm():
-            ident_bf16 = keep.tile([P, P], BF16)
-            nc.vector.tensor_copy(out=ident_bf16[:], in_=ident_f32[:])
-            bn_turned = turn_psum.tile([P, P], BF16, tag="turn")
-            nc.tensor.transpose(bn_turned[:], bn_rows[:], ident_bf16[:])
-            bn_cols = keep.tile([P, 4, CHUNKS], F32)
-            nc.vector.tensor_copy(out=bn_cols[:], in_=bn_turned[:, 0 : 4 * CHUNKS].rearrange("p (i cc) -> p i cc", i=4))
-            var_eps = keep.tile([P, CHUNKS], F32)
-            nc.vector.tensor_scalar_add(out=var_eps[:], in0=bn_cols[:, 3], scalar1=EPS)
-            std = keep.tile([P, CHUNKS], F32)
-            nc.scalar.sqrt(out=std[:], in_=var_eps[:])
+        bn_turned = turn_psum.tile([P, P], BF16, tag="turn")
+        nc.tensor.transpose(bn_turned[:], bn_rows[:], ident_bf16[:])
+        bn_cols = keep.tile([P, 4, CHUNKS], F32)
+        nc.scalar.copy(out=bn_cols[:], in_=bn_turned[:, 0 : 4 * CHUNKS].rearrange("p (i cc) -> p i cc", i=4))
+        std = keep.tile([P, CHUNKS], F32)
+        nc.scalar.activation(out=std[:], in_=bn_cols[:, 3], func=SQRT, bias=eps[:], scale=1.0)
+        bn_scale = keep.tile([P, CHUNKS], F32)
+        bn_shift = keep.tile([P, CHUNKS], F32)
+
+        def finish_batch_norm():
             inv_std = keep.tile([P, CHUNKS], F32)
             nc.vector.reciprocal(out=inv_std[:], in_=std[:])
-            bn_scale = keep.tile([P, CHUNKS], F32)
             nc.vector.tensor_mul(out=bn_scale[:], in0=bn_cols[:, 0], in1=inv_std[:])
             mean_scaled = keep.tile([P, CHUNKS], F32)
             nc.vector.tensor_mul(out=mean_scaled[:], in0=bn_cols[:, 2], in1=bn_scale[:])
-            bn_shift = keep.tile([P, CHUNKS], F32)
             nc.vector.tensor_sub(out=bn_shift[:], in0=bn_cols[:, 1], in1=mean_scaled[:])
-            return bn_scale, bn_shift
 
-        def first_passes(n, cc):
-            banks = []
-            for t in range(FRAMES):
-                joints = slice(t * JOINTS, (t + 1) * JOINTS)
-                acc = acc_psum.tile([P, WIDE], F32, tag="acc")
-                nc.tensor.matmul_mx(
-                    out=acc[:],
-                    lhsT=sp_codes[:, n, joints].bitcast(FP8X4),
-                    lhsT_scale=sp_scales[:, n, joints],
-                    rhs=w_codes[:, cc].bitcast(FP8X4),
-                    rhs_scale=w_scales[:, cc],
-                    start=True,
-                    stop=True,
-                )
-                banks.append(acc)
-            return banks
+        banks = {}
+        side_sums = {}
+        g_tiles = {}
 
-        def add_bias(acc, cc, g_frame):
-            nc.vector.tensor_tensor(out=g_frame, in0=acc[:], in1=bias_all[:, cc], op=ADD)
+        def first_pass(r, t, pool, tag):
+            n, cc = divmod(r, CHUNKS)
+            joints = slice(t * JOINTS, (t + 1) * JOINTS)
+            acc = pool.tile([P, WIDE], F32, tag=tag)
+            nc.tensor.matmul_mx(
+                out=acc[:],
+                lhsT=sp_codes[:, n, joints].bitcast(FP8X4),
+                lhsT_scale=sp_scales[:, n, joints],
+                rhs=w_codes[:, cc].bitcast(FP8X4),
+                rhs_scale=w_scales[:, cc],
+                start=True,
+                stop=True,
+            )
+            return acc
 
-        def second_layer(n, cc, g_grouped):
-            g_codes = work.tile([P, FRAMES, P], U32, align_bytes=64)
-            g_scales = work.tile([P, FRAMES, P], U8, align_bytes=64)
+        def refill(r, t):
+            if r < ROUNDS:
+                banks[(r, t)] = first_pass(r, t, acc_psum, "acc")
+
+        def side_copy(r):
+            if r < ROUNDS:
+                side_bank = first_pass(r, 0, side_psum, "side")
+                side_sum = work.tile([P, WIDE], F32)
+                nc.scalar.copy(out=side_sum[:], in_=side_bank[:])
+                side_sums[r] = side_sum
+
+        def side_add(r):
+            if r < ROUNDS:
+                g_grouped = work.tile([P, FRAMES, WIDE], BF16, align_bytes=64)
+                nc.gpsimd.tensor_tensor(out=g_grouped[:, 0], in0=side_sums[r][:], in1=bias_all[:, r % CHUNKS], op=ADD)
+                g_tiles[r] = g_grouped
+
+        def add_bias(r, t):
+            nc.vector.tensor_tensor(out=g_tiles[r][:, t], in0=banks[(r, t)][:], in1=bias_all[:, r % CHUNKS], op=ADD)
+
+        def second_layer(r, first, count):
+            n, cc = divmod(r, CHUNKS)
+            g_codes = work.tile([P, count, P], U32, align_bytes=64)
+            g_scales = work.tile([P, count, P], U8, align_bytes=64)
             nc.vector.quantize_mx(
                 out=g_codes[:].rearrange("v t c -> v (t c)").bitcast(FP8X4),
                 scales=g_scales[:].rearrange("v t c -> v (t c)"),
-                in_=g_grouped[:].rearrange("v t x -> v (t x)"),
+                in_=g_tiles[r][:, first : first + count].rearrange("v t x -> v (t x)"),
             )
-            y = y_psum.tile([P, FRAMES, JOINTS], F32)
-            for t in range(FRAMES):
+            y = y_psum.tile([P, count, JOINTS], F32)
+            for t in range(count):
                 nc.tensor.matmul_mx(
                     out=y[:, t],
                     lhsT=g_codes[:, t].bitcast(FP8X4),
@@ -177,7 +195,7 @@ def tile_ms_spatial_bottleneck_layer_pa_kernel(tc, sp_prev, spx, gcn_w, gcn_b, A
                     start=True,
                     stop=True,
                 )
-            result = work.tile([P, FRAMES * JOINTS], F32)
+            result = work.tile([P, count * JOINTS], F32)
             nc.scalar.activation(
                 out=result[:],
                 in_=y[:].rearrange("c t w -> c (t w)"),
@@ -185,24 +203,28 @@ def tile_ms_spatial_bottleneck_layer_pa_kernel(tc, sp_prev, spx, gcn_w, gcn_b, A
                 bias=bn_shift[:, cc : cc + 1],
                 scale=bn_scale[:, cc : cc + 1],
             )
-            nc.sync.dma_start(out=out[n, cc * P : (cc + 1) * P].rearrange("c t w -> c (t w)"), in_=result[:])
+            nc.sync.dma_start(
+                out=out[n, cc * P : (cc + 1) * P, first : first + count].rearrange("c t w -> c (t w)"), in_=result[:]
+            )
 
-        prepare_activations(0, nc.vector.tensor_copy)
-        prepare_weights(0)
-        prepare_activations(1, nc.scalar.copy)
-        bn_scale, bn_shift = prepare_batch_norm()
-
-        late = None
-        for cc in range(CHUNKS):
-            for n in range(BATCH):
-                banks = first_passes(n, cc)
-                g_grouped = work.tile([P, FRAMES, WIDE], BF16, align_bytes=64)
-                add_bias(banks[0], cc, g_grouped[:, 0])
-                if late is not None:
-                    second_layer(*late)
-                late = (n, cc, g_grouped)
-                if n == 0 and cc + 1 < CHUNKS:
-                    prepare_weights(cc + 1)
-                for t in range(1, FRAMES):
-                    add_bias(banks[t], cc, g_grouped[:, t])
-        second_layer(*late)
+        side_copy(0)
+        side_add(0)
+        for t in range(1, FRAMES):
+            refill(0, t)
+        side_copy(1)
+        for r in range(ROUNDS):
+            add_bias(r, 1)
+            refill(r + 1, 1)
+            if r == 0:
+                finish_batch_norm()
+            else:
+                second_layer(r - 1, 0, FRAMES)
+            side_add(r + 1)
+            add_bias(r, 2)
+            refill(r + 1, 2)
+            side_copy(r + 2)
+            if r == ROUNDS - 1:
+                second_layer(r, 0, FRAMES // 2)
+            add_bias(r, 3)
+            refill(r + 1, 3)
+        second_layer(ROUNDS - 1, FRAMES // 2, FRAMES // 2)

@@ -34,8 +34,9 @@ def tile_ms_spatial_bottleneck_layer_pa_kernel(tc, sp_prev, spx, gcn_w, gcn_b, A
         side_psum = stack.enter_context(tc.psum_pool(name="side_psum", bufs=1))
         turn_psum = stack.enter_context(tc.psum_pool(name="turn_psum", bufs=2))
         y_psum = stack.enter_context(tc.psum_pool(name="y_psum", bufs=2))
-        stack.enter_context(tc.manual_schedule())
 
+        ident_f32 = keep.tile([P, P], F32)
+        make_identity(nc, ident_f32[:])
         bn_rows = keep.tile([P, P], BF16)
         nc.vector.memset(bn_rows[:], 0.0)
         ones = keep.tile([P, P], BF16)
@@ -46,8 +47,6 @@ def tile_ms_spatial_bottleneck_layer_pa_kernel(tc, sp_prev, spx, gcn_w, gcn_b, A
         nc.scalar.sqrt(out=warm[:], in_=eps[:])
         for i, vec in enumerate((bg, bb, bm, bv)):
             nc.gpsimd.dma_start(out=bn_rows[CHUNKS * i : CHUNKS * (i + 1), :], in_=vec.rearrange("(cc p) -> cc p", p=P))
-        ident_f32 = keep.tile([P, P], F32)
-        make_identity(nc, ident_f32[:])
 
         bias_row = keep.tile([P, SUBSETS * CHANNELS], BF16)
         nc.vector.memset(bias_row[:].bitcast(I32), 0)
@@ -59,23 +58,42 @@ def tile_ms_spatial_bottleneck_layer_pa_kernel(tc, sp_prev, spx, gcn_w, gcn_b, A
                     out=raw[:, n].rearrange("q (u e) x -> q u (e x)", u=2),
                     in_=src[n].rearrange("(u q e) t v -> q u (e t v)", u=2, e=2),
                 )
+        w_raw = keep.tile([P, CHUNKS, SUBSETS, CHANNELS], BF16)
+        w_rows = gcn_w.rearrange("(k cc p) c -> cc p k c", k=SUBSETS, cc=CHUNKS)
+        nc.sync.dma_start(out=w_raw[:, 0], in_=w_rows[0])
         nc.sync.dma_start(out=bias_row[0:1, :], in_=gcn_b.unsqueeze(0))
         a_raw = keep.tile([P, SUBSETS, JOINTS], BF16)
         pa_raw = keep.tile([P, SUBSETS, JOINTS], BF16)
         nc.sync.dma_start(out=a_raw[:], in_=A.rearrange("k v w -> v k w"))
         nc.sync.dma_start(out=pa_raw[:], in_=PA.rearrange("k v w -> v k w"))
-        w_raw = keep.tile([P, CHUNKS, SUBSETS, CHANNELS], BF16)
-        w_rows = gcn_w.rearrange("(k cc p) c -> cc p k c", k=SUBSETS, cc=CHUNKS)
-        for cc in range(CHUNKS):
+        for cc in range(1, CHUNKS):
             nc.sync.dma_start(out=w_raw[:, cc], in_=w_rows[cc])
 
+        w_grouped = keep.tile([P, CHUNKS, WIDE * PACK], BF16, align_bytes=64)
+        w_codes = keep.tile([P, CHUNKS, WIDE], U32, align_bytes=64)
+        w_scales = keep.tile([P, CHUNKS, WIDE], U8, align_bytes=64)
         bias_all = keep.tile([P, CHUNKS, WIDE], BF16)
-        for cc in range(CHUNKS):
+
+        def turn_chunk(cc):
+            words_out = w_grouped[:, cc].bitcast(F32).rearrange("q (c k u) -> q c k u", k=SUBSETS, u=2)
+            for pair in range(SUBSETS // 2):
+                turned = turn_psum.tile([P, 2, 2, P], F32, tag="turn")
+                for k2 in range(2):
+                    for u in range(2):
+                        nc.tensor.transpose(
+                            turned[:, k2, u, :], w_raw[:, cc, 2 * pair + k2, :].bitcast(F32)[:, u * P : (u + 1) * P], ident_f32[:]
+                        )
+                nc.scalar.copy(out=words_out[:, :, 2 * pair : 2 * pair + 2, :], in_=turned[:].rearrange("q k u c -> q c k u"))
             spread = turn_psum.tile([P, P, SUBSETS], F32, tag="turn")
             for k in range(SUBSETS):
                 first = k * CHANNELS + cc * P
                 nc.tensor.matmul(spread[:, :, k], lhsT=ones[:], rhs=bias_row[:, first : first + P], start=True, stop=True)
             nc.scalar.copy(out=bias_all[:, cc], in_=spread[:].rearrange("p c k -> p (c k)"))
+
+        def quantise_chunk(cc):
+            nc.vector.quantize_mx(out=w_codes[:, cc].bitcast(FP8X4), scales=w_scales[:, cc], in_=w_grouped[:, cc])
+
+        turn_chunk(0)
 
         sp_sum = keep.tile([P, BATCH, PACK, TOKENS], BF16)
         sp_grouped = keep.tile([P, BATCH, TOKENS, PACK], BF16, align_bytes=64)
@@ -103,28 +121,9 @@ def tile_ms_spatial_bottleneck_layer_pa_kernel(tc, sp_prev, spx, gcn_w, gcn_b, A
         nc.vector.quantize_mx(
             out=adj_codes[:].bitcast(FP8X4), scales=adj_scales[:], in_=adj_grouped[:].rearrange("v w k -> v (w k)")
         )
+        quantise_chunk(0)
+        turn_chunk(1)
 
-        w_grouped = keep.tile([P, CHUNKS, WIDE * PACK], BF16, align_bytes=64)
-        w_codes = keep.tile([P, CHUNKS, WIDE], U32, align_bytes=64)
-        w_scales = keep.tile([P, CHUNKS, WIDE], U8, align_bytes=64)
-        for cc in range(CHUNKS):
-            words_out = w_grouped[:, cc].bitcast(F32).rearrange("q (c k u) -> q c k u", k=SUBSETS, u=2)
-            for pair in range(SUBSETS // 2):
-                turned = turn_psum.tile([P, 2, 2, P], F32, tag="turn")
-                for k2 in range(2):
-                    for u in range(2):
-                        nc.tensor.transpose(
-                            turned[:, k2, u, :], w_raw[:, cc, 2 * pair + k2, :].bitcast(F32)[:, u * P : (u + 1) * P], ident_f32[:]
-                        )
-                nc.scalar.copy(out=words_out[:, :, 2 * pair : 2 * pair + 2, :], in_=turned[:].rearrange("q k u c -> q c k u"))
-            nc.vector.quantize_mx(out=w_codes[:, cc].bitcast(FP8X4), scales=w_scales[:, cc], in_=w_grouped[:, cc])
-
-        bn_turned = turn_psum.tile([P, P], BF16, tag="turn")
-        nc.tensor.transpose(bn_turned[:], bn_rows[:], ident_bf16[:])
-        bn_cols = keep.tile([P, 4, CHUNKS], F32)
-        nc.scalar.copy(out=bn_cols[:], in_=bn_turned[:, 0 : 4 * CHUNKS].rearrange("p (i cc) -> p i cc", i=4))
-        std = keep.tile([P, CHUNKS], F32)
-        nc.scalar.activation(out=std[:], in_=bn_cols[:, 3], func=SQRT, bias=eps[:], scale=1.0)
         bn_scale = keep.tile([P, CHUNKS], F32)
         bn_shift = keep.tile([P, CHUNKS], F32)
 
@@ -141,7 +140,7 @@ def tile_ms_spatial_bottleneck_layer_pa_kernel(tc, sp_prev, spx, gcn_w, gcn_b, A
         g_tiles = {}
 
         def first_pass(r, t, pool, tag):
-            n, cc = divmod(r, CHUNKS)
+            cc, n = divmod(r, BATCH)
             joints = slice(t * JOINTS, (t + 1) * JOINTS)
             acc = pool.tile([P, WIDE], F32, tag=tag)
             nc.tensor.matmul_mx(
@@ -169,14 +168,14 @@ def tile_ms_spatial_bottleneck_layer_pa_kernel(tc, sp_prev, spx, gcn_w, gcn_b, A
         def side_add(r):
             if r < ROUNDS:
                 g_grouped = work.tile([P, FRAMES, WIDE], BF16, align_bytes=64)
-                nc.gpsimd.tensor_tensor(out=g_grouped[:, 0], in0=side_sums[r][:], in1=bias_all[:, r % CHUNKS], op=ADD)
+                nc.gpsimd.tensor_tensor(out=g_grouped[:, 0], in0=side_sums[r][:], in1=bias_all[:, r // BATCH], op=ADD)
                 g_tiles[r] = g_grouped
 
         def add_bias(r, t):
-            nc.vector.tensor_tensor(out=g_tiles[r][:, t], in0=banks[(r, t)][:], in1=bias_all[:, r % CHUNKS], op=ADD)
+            nc.vector.tensor_tensor(out=g_tiles[r][:, t], in0=banks[(r, t)][:], in1=bias_all[:, r // BATCH], op=ADD)
 
         def second_layer(r, first, count):
-            n, cc = divmod(r, CHUNKS)
+            cc, n = divmod(r, BATCH)
             g_codes = work.tile([P, count, P], U32, align_bytes=64)
             g_scales = work.tile([P, count, P], U8, align_bytes=64)
             nc.vector.quantize_mx(
@@ -212,13 +211,20 @@ def tile_ms_spatial_bottleneck_layer_pa_kernel(tc, sp_prev, spx, gcn_w, gcn_b, A
         for t in range(1, FRAMES):
             refill(0, t)
         side_copy(1)
+        bn_turned = turn_psum.tile([P, P], BF16, tag="turn")
+        nc.tensor.transpose(bn_turned[:], bn_rows[:], ident_bf16[:])
+        bn_cols = keep.tile([P, 4, CHUNKS], F32)
+        nc.scalar.copy(out=bn_cols[:], in_=bn_turned[:, 0 : 4 * CHUNKS].rearrange("p (i cc) -> p i cc", i=4))
+        std = keep.tile([P, CHUNKS], F32)
+        nc.scalar.activation(out=std[:], in_=bn_cols[:, 3], func=SQRT, bias=eps[:], scale=1.0)
         for r in range(ROUNDS):
+            cc, n = divmod(r, BATCH)
             add_bias(r, 1)
             refill(r + 1, 1)
-            if r == 0:
-                finish_batch_norm()
-            else:
+            if r > 0:
                 second_layer(r - 1, 0, FRAMES)
+            if n == 0 and cc + 1 < CHUNKS:
+                quantise_chunk(cc + 1)
             side_add(r + 1)
             add_bias(r, 2)
             refill(r + 1, 2)
@@ -227,4 +233,8 @@ def tile_ms_spatial_bottleneck_layer_pa_kernel(tc, sp_prev, spx, gcn_w, gcn_b, A
                 second_layer(r, 0, FRAMES // 2)
             add_bias(r, 3)
             refill(r + 1, 3)
+            if r == 0:
+                finish_batch_norm()
+            if n == 1 and cc + 2 < CHUNKS:
+                turn_chunk(cc + 2)
         second_layer(ROUNDS - 1, FRAMES // 2, FRAMES // 2)

@@ -29,7 +29,8 @@ def tile_ms_spatial_bottleneck_layer_pa_kernel(tc, sp_prev, spx, gcn_w, gcn_b, A
     nc = tc.nc
     with ExitStack() as stack:
         keep = stack.enter_context(tc.tile_pool(name="keep", bufs=1))
-        work = stack.enter_context(tc.tile_pool(name="work", bufs=2))
+        work = stack.enter_context(tc.tile_pool(name="work", bufs=4))
+        g_pool = stack.enter_context(tc.tile_pool(name="g_pool", bufs=2))
         acc_psum = stack.enter_context(tc.psum_pool(name="acc_psum", bufs=FRAMES - 1))
         side_psum = stack.enter_context(tc.psum_pool(name="side_psum", bufs=1))
         turn_psum = stack.enter_context(tc.psum_pool(name="turn_psum", bufs=2))
@@ -52,20 +53,24 @@ def tile_ms_spatial_bottleneck_layer_pa_kernel(tc, sp_prev, spx, gcn_w, gcn_b, A
         nc.vector.memset(bias_row[:].bitcast(I32), 0)
         prev_raw = keep.tile([P, BATCH, PACK, TOKENS], BF16)
         x_raw = keep.tile([P, BATCH, PACK, TOKENS], BF16)
-        for n in range(BATCH):
+        a_raw = keep.tile([P, SUBSETS, JOINTS], BF16)
+        pa_raw = keep.tile([P, SUBSETS, JOINTS], BF16)
+        nc.sync.dma_start(out=a_raw[:], in_=A.rearrange("k v w -> v k w"))
+        nc.sync.dma_start(out=pa_raw[:], in_=PA.rearrange("k v w -> v k w"))
+
+        def load_activations(n):
             for raw, src in ((prev_raw, sp_prev), (x_raw, spx)):
                 nc.sync.dma_start(
                     out=raw[:, n].rearrange("q (u e) x -> q u (e x)", u=2),
                     in_=src[n].rearrange("(u q e) t v -> q u (e t v)", u=2, e=2),
                 )
+
         w_raw = keep.tile([P, CHUNKS, SUBSETS, CHANNELS], BF16)
         w_rows = gcn_w.rearrange("(k cc p) c -> cc p k c", k=SUBSETS, cc=CHUNKS)
+        load_activations(0)
         nc.sync.dma_start(out=w_raw[:, 0], in_=w_rows[0])
         nc.sync.dma_start(out=bias_row[0:1, :], in_=gcn_b.unsqueeze(0))
-        a_raw = keep.tile([P, SUBSETS, JOINTS], BF16)
-        pa_raw = keep.tile([P, SUBSETS, JOINTS], BF16)
-        nc.sync.dma_start(out=a_raw[:], in_=A.rearrange("k v w -> v k w"))
-        nc.sync.dma_start(out=pa_raw[:], in_=PA.rearrange("k v w -> v k w"))
+        load_activations(1)
         for cc in range(1, CHUNKS):
             nc.sync.dma_start(out=w_raw[:, cc], in_=w_rows[cc])
 
@@ -95,21 +100,6 @@ def tile_ms_spatial_bottleneck_layer_pa_kernel(tc, sp_prev, spx, gcn_w, gcn_b, A
 
         turn_chunk(0)
 
-        sp_sum = keep.tile([P, BATCH, PACK, TOKENS], BF16)
-        sp_grouped = keep.tile([P, BATCH, TOKENS, PACK], BF16, align_bytes=64)
-        sp_codes = keep.tile([P, BATCH, TOKENS], U32, align_bytes=64)
-        sp_scales = keep.tile([P, BATCH, TOKENS], U8, align_bytes=64)
-        for n in range(BATCH):
-            nc.vector.tensor_tensor(out=sp_sum[:, n], in0=prev_raw[:, n], in1=x_raw[:, n], op=ADD)
-            nc.vector.tensor_copy(
-                out=sp_grouped[:, n].rearrange("q (x i) j -> q x j i", i=4),
-                in_=sp_sum[:, n].rearrange("q j (x i) -> q x j i", i=4),
-            )
-        for n in range(BATCH):
-            nc.vector.quantize_mx(
-                out=sp_codes[:, n].bitcast(FP8X4), scales=sp_scales[:, n], in_=sp_grouped[:, n].rearrange("q x j -> q (x j)")
-            )
-
         adj_sum = keep.tile([P, SUBSETS, JOINTS], BF16)
         nc.vector.tensor_tensor(out=adj_sum[:], in0=a_raw[:], in1=pa_raw[:], op=ADD)
         adj_grouped = keep.tile([P, JOINTS, SUBSETS], BF16, align_bytes=64)
@@ -121,6 +111,24 @@ def tile_ms_spatial_bottleneck_layer_pa_kernel(tc, sp_prev, spx, gcn_w, gcn_b, A
         nc.vector.quantize_mx(
             out=adj_codes[:].bitcast(FP8X4), scales=adj_scales[:], in_=adj_grouped[:].rearrange("v w k -> v (w k)")
         )
+
+        sp_sum = keep.tile([P, BATCH, PACK, TOKENS], BF16)
+        sp_grouped = keep.tile([P, BATCH, TOKENS, PACK], BF16, align_bytes=64)
+        sp_codes = keep.tile([P, BATCH, TOKENS], U32, align_bytes=64)
+        sp_scales = keep.tile([P, BATCH, TOKENS], U8, align_bytes=64)
+
+        def prepare_activations(n):
+            nc.vector.tensor_tensor(out=sp_sum[:, n], in0=prev_raw[:, n], in1=x_raw[:, n], op=ADD)
+            nc.vector.tensor_copy(
+                out=sp_grouped[:, n].rearrange("q (x i) j -> q x j i", i=4),
+                in_=sp_sum[:, n].rearrange("q j (x i) -> q x j i", i=4),
+            )
+            nc.vector.quantize_mx(
+                out=sp_codes[:, n].bitcast(FP8X4), scales=sp_scales[:, n], in_=sp_grouped[:, n].rearrange("q x j -> q (x j)")
+            )
+
+        prepare_activations(0)
+
         quantise_chunk(0)
         turn_chunk(1)
 
@@ -167,7 +175,7 @@ def tile_ms_spatial_bottleneck_layer_pa_kernel(tc, sp_prev, spx, gcn_w, gcn_b, A
 
         def side_add(r):
             if r < ROUNDS:
-                g_grouped = work.tile([P, FRAMES, WIDE], BF16, align_bytes=64)
+                g_grouped = g_pool.tile([P, FRAMES, WIDE], BF16, align_bytes=64)
                 nc.gpsimd.tensor_tensor(out=g_grouped[:, 0], in0=side_sums[r][:], in1=bias_all[:, r // BATCH], op=ADD)
                 g_tiles[r] = g_grouped
 
@@ -210,6 +218,7 @@ def tile_ms_spatial_bottleneck_layer_pa_kernel(tc, sp_prev, spx, gcn_w, gcn_b, A
         side_add(0)
         for t in range(1, FRAMES):
             refill(0, t)
+        prepare_activations(1)
         side_copy(1)
         bn_turned = turn_psum.tile([P, P], BF16, tag="turn")
         nc.tensor.transpose(bn_turned[:], bn_rows[:], ident_bf16[:])

@@ -5,7 +5,6 @@ from concourse.masks import make_identity
 
 BF16 = mybir.dt.bfloat16
 F32 = mybir.dt.float32
-I32 = mybir.dt.int32
 U32 = mybir.dt.uint32
 U8 = mybir.dt.uint8
 FP8X4 = mybir.dt.float8_e4m3fn_x4
@@ -19,7 +18,9 @@ BATCH, FRAMES, JOINTS, SUBSETS, CHANNELS = 2, 4, 128, 4, 512
 CHUNKS = CHANNELS // P
 TOKENS = FRAMES * JOINTS
 WIDE = P * SUBSETS
-ROUNDS = BATCH * CHUNKS
+ROUND_LIST = [(0, 0), (1, 0), (0, 1), (1, 1), (2, 0), (2, 1), (3, 0), (3, 1)]
+ROUNDS = len(ROUND_LIST)
+BIAS_RUN = SUBSETS * CHANNELS // P
 EPS = 1e-5
 
 FLOPS = 2 * BATCH * TOKENS * SUBSETS * CHANNELS * CHANNELS + 2 * BATCH * FRAMES * CHANNELS * SUBSETS * JOINTS * JOINTS
@@ -36,27 +37,23 @@ def tile_ms_spatial_bottleneck_layer_pa_kernel(tc, sp_prev, spx, gcn_w, gcn_b, A
         turn_psum = stack.enter_context(tc.psum_pool(name="turn_psum", bufs=2))
         y_psum = stack.enter_context(tc.psum_pool(name="y_psum", bufs=2))
 
+        ident_bf16 = keep.tile([P, P], BF16)
+        make_identity(nc, ident_bf16[:])
         ident_f32 = keep.tile([P, P], F32)
         make_identity(nc, ident_f32[:])
         bn_rows = keep.tile([P, P], BF16)
         nc.vector.memset(bn_rows[:], 0.0)
-        ones = keep.tile([P, P], BF16)
-        nc.vector.memset(ones[:], 1.0)
         eps = keep.tile([P, 1], F32)
         nc.vector.memset(eps[:], EPS)
         warm = keep.tile([P, 1], F32)
         nc.scalar.sqrt(out=warm[:], in_=eps[:])
-        for i, vec in enumerate((bg, bb, bm, bv)):
-            nc.gpsimd.dma_start(out=bn_rows[CHUNKS * i : CHUNKS * (i + 1), :], in_=vec.rearrange("(cc p) -> cc p", p=P))
 
-        bias_row = keep.tile([P, SUBSETS * CHANNELS], BF16)
-        nc.vector.memset(bias_row[:].bitcast(I32), 0)
+        bias_runs = keep.tile([P, BIAS_RUN], BF16)
+        nc.sync.dma_start(out=bias_runs[:], in_=gcn_b.rearrange("(p m) -> p m", m=BIAS_RUN))
         prev_raw = keep.tile([P, BATCH, PACK, TOKENS], BF16)
         x_raw = keep.tile([P, BATCH, PACK, TOKENS], BF16)
         a_raw = keep.tile([P, SUBSETS, JOINTS], BF16)
         pa_raw = keep.tile([P, SUBSETS, JOINTS], BF16)
-        nc.sync.dma_start(out=a_raw[:], in_=A.rearrange("k v w -> v k w"))
-        nc.sync.dma_start(out=pa_raw[:], in_=PA.rearrange("k v w -> v k w"))
 
         def load_activations(n):
             for raw, src in ((prev_raw, sp_prev), (x_raw, spx)):
@@ -67,17 +64,21 @@ def tile_ms_spatial_bottleneck_layer_pa_kernel(tc, sp_prev, spx, gcn_w, gcn_b, A
 
         w_raw = keep.tile([P, CHUNKS, SUBSETS, CHANNELS], BF16)
         w_rows = gcn_w.rearrange("(k cc p) c -> cc p k c", k=SUBSETS, cc=CHUNKS)
-        load_activations(0)
         nc.sync.dma_start(out=w_raw[:, 0], in_=w_rows[0])
-        nc.sync.dma_start(out=bias_row[0:1, :], in_=gcn_b.unsqueeze(0))
+        nc.sync.dma_start(out=a_raw[:], in_=A.rearrange("k v w -> v k w"))
+        nc.sync.dma_start(out=pa_raw[:], in_=PA.rearrange("k v w -> v k w"))
+        load_activations(0)
+        nc.sync.dma_start(out=w_raw[:, 1], in_=w_rows[1])
         load_activations(1)
-        for cc in range(1, CHUNKS):
+        for i, vec in enumerate((bg, bb, bm, bv)):
+            nc.sync.dma_start(out=bn_rows[CHUNKS * i : CHUNKS * (i + 1), :], in_=vec.rearrange("(cc p) -> cc p", p=P))
+        for cc in range(2, CHUNKS):
             nc.sync.dma_start(out=w_raw[:, cc], in_=w_rows[cc])
 
         w_grouped = keep.tile([P, CHUNKS, WIDE * PACK], BF16, align_bytes=64)
         w_codes = keep.tile([P, CHUNKS, WIDE], U32, align_bytes=64)
         w_scales = keep.tile([P, CHUNKS, WIDE], U8, align_bytes=64)
-        bias_all = keep.tile([P, CHUNKS, WIDE], BF16)
+        bias_all = keep.tile([P, CHUNKS * WIDE], BF16)
 
         def turn_chunk(cc):
             words_out = w_grouped[:, cc].bitcast(F32).rearrange("q (c k u) -> q c k u", k=SUBSETS, u=2)
@@ -89,14 +90,21 @@ def tile_ms_spatial_bottleneck_layer_pa_kernel(tc, sp_prev, spx, gcn_w, gcn_b, A
                             turned[:, k2, u, :], w_raw[:, cc, 2 * pair + k2, :].bitcast(F32)[:, u * P : (u + 1) * P], ident_f32[:]
                         )
                 nc.scalar.copy(out=words_out[:, :, 2 * pair : 2 * pair + 2, :], in_=turned[:].rearrange("q k u c -> q c k u"))
-            spread = turn_psum.tile([P, P, SUBSETS], F32, tag="turn")
-            for k in range(SUBSETS):
-                first = k * CHANNELS + cc * P
-                nc.tensor.matmul(spread[:, :, k], lhsT=ones[:], rhs=bias_row[:, first : first + P], start=True, stop=True)
-            nc.scalar.copy(out=bias_all[:, cc], in_=spread[:].rearrange("p c k -> p (c k)"))
 
         def quantise_chunk(cc):
             nc.vector.quantize_mx(out=w_codes[:, cc].bitcast(FP8X4), scales=w_scales[:, cc], in_=w_grouped[:, cc])
+
+        per_bank = BIAS_RUN // 2
+        bias_out = bias_all[:].rearrange("p (x m k) -> p x m k", m=BIAS_RUN, k=SUBSETS)
+        for half in range(2):
+            spread = turn_psum.tile([P, per_bank, P], BF16, tag="turn")
+            for m in range(per_bank):
+                first = half * per_bank + m
+                nc.tensor.transpose(spread[:, m, :], bias_runs[:, first : first + 1].to_broadcast([P, P]), ident_bf16[:])
+            nc.scalar.copy(
+                out=bias_out[:, :, half * per_bank : (half + 1) * per_bank, :],
+                in_=spread[:].rearrange("p m (k x) -> p x m k", k=SUBSETS),
+            )
 
         turn_chunk(0)
 
@@ -104,32 +112,39 @@ def tile_ms_spatial_bottleneck_layer_pa_kernel(tc, sp_prev, spx, gcn_w, gcn_b, A
         nc.vector.tensor_tensor(out=adj_sum[:], in0=a_raw[:], in1=pa_raw[:], op=ADD)
         adj_grouped = keep.tile([P, JOINTS, SUBSETS], BF16, align_bytes=64)
         nc.vector.tensor_copy(out=adj_grouped[:], in_=adj_sum[:].rearrange("v k w -> v w k"))
-        ident_bf16 = keep.tile([P, P], BF16)
-        nc.vector.tensor_copy(out=ident_bf16[:], in_=ident_f32[:])
         adj_codes = keep.tile([P, JOINTS], U32, align_bytes=64)
         adj_scales = keep.tile([P, JOINTS], U8, align_bytes=64)
         nc.vector.quantize_mx(
             out=adj_codes[:].bitcast(FP8X4), scales=adj_scales[:], in_=adj_grouped[:].rearrange("v w k -> v (w k)")
         )
 
-        sp_sum = keep.tile([P, BATCH, PACK, TOKENS], BF16)
         sp_grouped = keep.tile([P, BATCH, TOKENS, PACK], BF16, align_bytes=64)
         sp_codes = keep.tile([P, BATCH, TOKENS], U32, align_bytes=64)
         sp_scales = keep.tile([P, BATCH, TOKENS], U8, align_bytes=64)
 
-        def prepare_activations(n):
-            nc.vector.tensor_tensor(out=sp_sum[:, n], in0=prev_raw[:, n], in1=x_raw[:, n], op=ADD)
-            nc.vector.tensor_copy(
-                out=sp_grouped[:, n].rearrange("q (x i) j -> q x j i", i=4),
-                in_=sp_sum[:, n].rearrange("q j (x i) -> q x j i", i=4),
-            )
-            nc.vector.quantize_mx(
-                out=sp_codes[:, n].bitcast(FP8X4), scales=sp_scales[:, n], in_=sp_grouped[:, n].rearrange("q x j -> q (x j)")
-            )
+        def add_frame(n, t, pool, tag, copy):
+            joints = slice(t * JOINTS, (t + 1) * JOINTS)
+            total = pool.tile([P, PACK, JOINTS], F32, tag=tag)
+            nc.tensor.matmul(total[:], lhsT=ident_bf16[:], rhs=prev_raw[:, n, :, joints], start=True, stop=False)
+            nc.tensor.matmul(total[:], lhsT=ident_bf16[:], rhs=x_raw[:, n, :, joints], start=False, stop=True)
+            copy(out=sp_grouped[:, n, joints], in_=total[:].rearrange("q j v -> q v j"))
 
-        prepare_activations(0)
+        def quantise_frames(n, first, count):
+            joints = slice(first * JOINTS, (first + count) * JOINTS)
+            nc.vector.quantize_mx(
+                out=sp_codes[:, n, joints].bitcast(FP8X4),
+                scales=sp_scales[:, n, joints],
+                in_=sp_grouped[:, n, joints].rearrange("q x j -> q (x j)"),
+            )
 
         quantise_chunk(0)
+        add_frame(0, 0, y_psum, "y", nc.vector.tensor_copy)
+        add_frame(0, 1, y_psum, "y", nc.scalar.copy)
+        add_frame(0, 2, acc_psum, "acc", nc.vector.tensor_copy)
+        add_frame(0, 3, acc_psum, "acc", nc.scalar.copy)
+        for t in range(FRAMES):
+            quantise_frames(0, t, 1)
+
         turn_chunk(1)
 
         bn_scale = keep.tile([P, CHUNKS], F32)
@@ -147,8 +162,12 @@ def tile_ms_spatial_bottleneck_layer_pa_kernel(tc, sp_prev, spx, gcn_w, gcn_b, A
         side_sums = {}
         g_tiles = {}
 
+        def bias_of(r):
+            cc = ROUND_LIST[r][0]
+            return bias_all[:, cc * WIDE : (cc + 1) * WIDE]
+
         def first_pass(r, t, pool, tag):
-            cc, n = divmod(r, BATCH)
+            cc, n = ROUND_LIST[r]
             joints = slice(t * JOINTS, (t + 1) * JOINTS)
             acc = pool.tile([P, WIDE], F32, tag=tag)
             nc.tensor.matmul_mx(
@@ -176,14 +195,14 @@ def tile_ms_spatial_bottleneck_layer_pa_kernel(tc, sp_prev, spx, gcn_w, gcn_b, A
         def side_add(r):
             if r < ROUNDS:
                 g_grouped = g_pool.tile([P, FRAMES, WIDE], BF16, align_bytes=64)
-                nc.gpsimd.tensor_tensor(out=g_grouped[:, 0], in0=side_sums[r][:], in1=bias_all[:, r // BATCH], op=ADD)
+                nc.gpsimd.tensor_tensor(out=g_grouped[:, 0], in0=side_sums[r][:], in1=bias_of(r), op=ADD)
                 g_tiles[r] = g_grouped
 
         def add_bias(r, t):
-            nc.vector.tensor_tensor(out=g_tiles[r][:, t], in0=banks[(r, t)][:], in1=bias_all[:, r // BATCH], op=ADD)
+            nc.vector.tensor_tensor(out=g_tiles[r][:, t], in0=banks[(r, t)][:], in1=bias_of(r), op=ADD)
 
         def second_layer(r, first, count):
-            cc, n = divmod(r, BATCH)
+            cc, n = ROUND_LIST[r]
             g_codes = work.tile([P, count, P], U32, align_bytes=64)
             g_scales = work.tile([P, count, P], U8, align_bytes=64)
             nc.vector.quantize_mx(
@@ -191,7 +210,7 @@ def tile_ms_spatial_bottleneck_layer_pa_kernel(tc, sp_prev, spx, gcn_w, gcn_b, A
                 scales=g_scales[:].rearrange("v t c -> v (t c)"),
                 in_=g_tiles[r][:, first : first + count].rearrange("v t x -> v (t x)"),
             )
-            y = y_psum.tile([P, count, JOINTS], F32)
+            y = y_psum.tile([P, count, JOINTS], F32, tag="y")
             for t in range(count):
                 nc.tensor.matmul_mx(
                     out=y[:, t],
@@ -218,22 +237,39 @@ def tile_ms_spatial_bottleneck_layer_pa_kernel(tc, sp_prev, spx, gcn_w, gcn_b, A
         side_add(0)
         for t in range(1, FRAMES):
             refill(0, t)
-        prepare_activations(1)
+        for t in range(1, FRAMES):
+            add_bias(0, t)
+        quantise_chunk(1)
         side_copy(1)
+        side_add(1)
+        for t in range(1, FRAMES):
+            refill(1, t)
+        for t in range(FRAMES):
+            add_frame(1, t, y_psum, "y", nc.scalar.copy)
         bn_turned = turn_psum.tile([P, P], BF16, tag="turn")
         nc.tensor.transpose(bn_turned[:], bn_rows[:], ident_bf16[:])
         bn_cols = keep.tile([P, 4, CHUNKS], F32)
         nc.scalar.copy(out=bn_cols[:], in_=bn_turned[:, 0 : 4 * CHUNKS].rearrange("p (i cc) -> p i cc", i=4))
         std = keep.tile([P, CHUNKS], F32)
         nc.scalar.activation(out=std[:], in_=bn_cols[:, 3], func=SQRT, bias=eps[:], scale=1.0)
-        for r in range(ROUNDS):
-            cc, n = divmod(r, BATCH)
+        finish_batch_norm()
+        add_bias(1, 1)
+        add_bias(1, 2)
+        second_layer(0, 0, FRAMES)
+        quantise_frames(1, 0, FRAMES)
+        add_bias(1, 3)
+        side_copy(2)
+        side_add(2)
+        for t in range(1, FRAMES):
+            refill(2, t)
+        side_copy(3)
+        turn_chunk(2)
+        for r in range(2, ROUNDS):
             add_bias(r, 1)
             refill(r + 1, 1)
-            if r > 0:
-                second_layer(r - 1, 0, FRAMES)
-            if n == 0 and cc + 1 < CHUNKS:
-                quantise_chunk(cc + 1)
+            second_layer(r - 1, 0, FRAMES)
+            if r == 2 or r == 4:
+                quantise_chunk(r // 2 + 1)
             side_add(r + 1)
             add_bias(r, 2)
             refill(r + 1, 2)
@@ -242,8 +278,6 @@ def tile_ms_spatial_bottleneck_layer_pa_kernel(tc, sp_prev, spx, gcn_w, gcn_b, A
                 second_layer(r, 0, FRAMES // 2)
             add_bias(r, 3)
             refill(r + 1, 3)
-            if r == 0:
-                finish_batch_norm()
-            if n == 1 and cc + 2 < CHUNKS:
-                turn_chunk(cc + 2)
+            if r == 3:
+                turn_chunk(3)
         second_layer(ROUNDS - 1, FRAMES // 2, FRAMES // 2)

@@ -37,6 +37,7 @@ def tile_ms_spatial_bottleneck_layer_pa_kernel(tc, sp_prev, spx, gcn_w, gcn_b, A
         turn_psum = stack.enter_context(tc.psum_pool(name="turn_psum", bufs=2))
         y_psum = stack.enter_context(tc.psum_pool(name="y_psum", bufs=2))
 
+        stack.enter_context(tc.manual_schedule())
         ident_bf16 = keep.tile([P, P], BF16)
         make_identity(nc, ident_bf16[:])
         ident_f32 = keep.tile([P, P], F32)
@@ -69,9 +70,9 @@ def tile_ms_spatial_bottleneck_layer_pa_kernel(tc, sp_prev, spx, gcn_w, gcn_b, A
         nc.sync.dma_start(out=pa_raw[:], in_=PA.rearrange("k v w -> v k w"))
         load_activations(0)
         nc.sync.dma_start(out=w_raw[:, 1], in_=w_rows[1])
-        load_activations(1)
         for i, vec in enumerate((bg, bb, bm, bv)):
             nc.sync.dma_start(out=bn_rows[CHUNKS * i : CHUNKS * (i + 1), :], in_=vec.rearrange("(cc p) -> cc p", p=P))
+        load_activations(1)
         for cc in range(2, CHUNKS):
             nc.sync.dma_start(out=w_raw[:, cc], in_=w_rows[cc])
 
@@ -80,44 +81,47 @@ def tile_ms_spatial_bottleneck_layer_pa_kernel(tc, sp_prev, spx, gcn_w, gcn_b, A
         w_scales = keep.tile([P, CHUNKS, WIDE], U8, align_bytes=64)
         bias_all = keep.tile([P, CHUNKS * WIDE], BF16)
 
-        def turn_chunk(cc):
+        def turn_pair(cc, pair):
             words_out = w_grouped[:, cc].bitcast(F32).rearrange("q (c k u) -> q c k u", k=SUBSETS, u=2)
-            for pair in range(SUBSETS // 2):
-                turned = turn_psum.tile([P, 2, 2, P], F32, tag="turn")
-                for k2 in range(2):
-                    for u in range(2):
-                        nc.tensor.transpose(
-                            turned[:, k2, u, :], w_raw[:, cc, 2 * pair + k2, :].bitcast(F32)[:, u * P : (u + 1) * P], ident_f32[:]
-                        )
-                nc.scalar.copy(out=words_out[:, :, 2 * pair : 2 * pair + 2, :], in_=turned[:].rearrange("q k u c -> q c k u"))
+            turned = turn_psum.tile([P, 2, 2, P], F32, tag="turn")
+            for k2 in range(2):
+                for u in range(2):
+                    nc.tensor.transpose(
+                        turned[:, k2, u, :], w_raw[:, cc, 2 * pair + k2, :].bitcast(F32)[:, u * P : (u + 1) * P], ident_f32[:]
+                    )
+            nc.scalar.copy(out=words_out[:, :, 2 * pair : 2 * pair + 2, :], in_=turned[:].rearrange("q k u c -> q c k u"))
 
         def quantise_chunk(cc):
             nc.vector.quantize_mx(out=w_codes[:, cc].bitcast(FP8X4), scales=w_scales[:, cc], in_=w_grouped[:, cc])
 
         per_bank = BIAS_RUN // 2
         bias_out = bias_all[:].rearrange("p (x m k) -> p x m k", m=BIAS_RUN, k=SUBSETS)
-        for half in range(2):
+
+        def spread_bias(half):
             spread = turn_psum.tile([P, per_bank, P], BF16, tag="turn")
             for m in range(per_bank):
                 first = half * per_bank + m
-                nc.tensor.transpose(spread[:, m, :], bias_runs[:, first : first + 1].to_broadcast([P, P]), ident_bf16[:])
+                nc.tensor.matmul(
+                    spread[:, m, :], lhsT=bias_runs[:, first : first + 1].to_broadcast([P, P]), rhs=ident_bf16[:], start=True, stop=True
+                )
             nc.scalar.copy(
                 out=bias_out[:, :, half * per_bank : (half + 1) * per_bank, :],
                 in_=spread[:].rearrange("p m (k x) -> p x m k", k=SUBSETS),
             )
 
-        turn_chunk(0)
-
         adj_sum = keep.tile([P, SUBSETS, JOINTS], BF16)
-        nc.vector.tensor_tensor(out=adj_sum[:], in0=a_raw[:], in1=pa_raw[:], op=ADD)
         adj_grouped = keep.tile([P, JOINTS, SUBSETS], BF16, align_bytes=64)
-        nc.vector.tensor_copy(out=adj_grouped[:], in_=adj_sum[:].rearrange("v k w -> v w k"))
         adj_codes = keep.tile([P, JOINTS], U32, align_bytes=64)
         adj_scales = keep.tile([P, JOINTS], U8, align_bytes=64)
-        nc.vector.quantize_mx(
-            out=adj_codes[:].bitcast(FP8X4), scales=adj_scales[:], in_=adj_grouped[:].rearrange("v w k -> v (w k)")
-        )
 
+        def prepare_adjacency():
+            nc.vector.tensor_tensor(out=adj_sum[:], in0=a_raw[:], in1=pa_raw[:], op=ADD)
+            nc.vector.tensor_copy(out=adj_grouped[:], in_=adj_sum[:].rearrange("v k w -> v w k"))
+            nc.vector.quantize_mx(
+                out=adj_codes[:].bitcast(FP8X4), scales=adj_scales[:], in_=adj_grouped[:].rearrange("v w k -> v (w k)")
+            )
+
+        sp_sum = keep.tile([P, PACK, TOKENS], BF16)
         sp_grouped = keep.tile([P, BATCH, TOKENS, PACK], BF16, align_bytes=64)
         sp_codes = keep.tile([P, BATCH, TOKENS], U32, align_bytes=64)
         sp_scales = keep.tile([P, BATCH, TOKENS], U8, align_bytes=64)
@@ -129,6 +133,17 @@ def tile_ms_spatial_bottleneck_layer_pa_kernel(tc, sp_prev, spx, gcn_w, gcn_b, A
             nc.tensor.matmul(total[:], lhsT=ident_bf16[:], rhs=x_raw[:, n, :, joints], start=False, stop=True)
             copy(out=sp_grouped[:, n, joints], in_=total[:].rearrange("q j v -> q v j"))
 
+        def sum_frame(t):
+            joints = slice(t * JOINTS, (t + 1) * JOINTS)
+            nc.vector.tensor_tensor(out=sp_sum[:, :, joints], in0=prev_raw[:, 0, :, joints], in1=x_raw[:, 0, :, joints], op=ADD)
+
+        def interleave_frame(t):
+            joints = slice(t * JOINTS, (t + 1) * JOINTS)
+            nc.vector.tensor_copy(
+                out=sp_grouped[:, 0, joints].rearrange("q (x i) j -> q x j i", i=4),
+                in_=sp_sum[:, :, joints].rearrange("q j (x i) -> q x j i", i=4),
+            )
+
         def quantise_frames(n, first, count):
             joints = slice(first * JOINTS, (first + count) * JOINTS)
             nc.vector.quantize_mx(
@@ -137,31 +152,29 @@ def tile_ms_spatial_bottleneck_layer_pa_kernel(tc, sp_prev, spx, gcn_w, gcn_b, A
                 in_=sp_grouped[:, n, joints].rearrange("q x j -> q (x j)"),
             )
 
-        quantise_chunk(0)
-        add_frame(0, 0, y_psum, "y", nc.vector.tensor_copy)
-        add_frame(0, 1, y_psum, "y", nc.scalar.copy)
-        add_frame(0, 2, acc_psum, "acc", nc.vector.tensor_copy)
-        add_frame(0, 3, acc_psum, "acc", nc.scalar.copy)
-        for t in range(FRAMES):
-            quantise_frames(0, t, 1)
-
-        turn_chunk(1)
-
         bn_scale = keep.tile([P, CHUNKS], F32)
         bn_shift = keep.tile([P, CHUNKS], F32)
+        bn_cols = keep.tile([P, 4, CHUNKS], F32)
+        std = keep.tile([P, CHUNKS], F32)
+
+        def start_batch_norm():
+            bn_turned = turn_psum.tile([P, P], BF16, tag="turn")
+            nc.tensor.transpose(bn_turned[:], bn_rows[:], ident_bf16[:])
+            nc.scalar.copy(out=bn_cols[:], in_=bn_turned[:, 0 : 4 * CHUNKS].rearrange("p (i cc) -> p i cc", i=4))
+            nc.scalar.activation(out=std[:], in_=bn_cols[:, 3], func=SQRT, bias=eps[:], scale=1.0)
+
+        inv_std = keep.tile([P, CHUNKS], F32)
+        mean_scaled = keep.tile([P, CHUNKS], F32)
 
         def finish_batch_norm():
-            inv_std = keep.tile([P, CHUNKS], F32)
             nc.vector.reciprocal(out=inv_std[:], in_=std[:])
-            nc.vector.tensor_mul(out=bn_scale[:], in0=bn_cols[:, 0], in1=inv_std[:])
-            mean_scaled = keep.tile([P, CHUNKS], F32)
-            nc.vector.tensor_mul(out=mean_scaled[:], in0=bn_cols[:, 2], in1=bn_scale[:])
-            nc.vector.tensor_sub(out=bn_shift[:], in0=bn_cols[:, 1], in1=mean_scaled[:])
+            nc.gpsimd.tensor_mul(out=bn_scale[:], in0=bn_cols[:, 0], in1=inv_std[:])
+            nc.gpsimd.tensor_mul(out=mean_scaled[:], in0=bn_cols[:, 2], in1=bn_scale[:])
+            nc.gpsimd.tensor_sub(out=bn_shift[:], in0=bn_cols[:, 1], in1=mean_scaled[:])
 
         banks = {}
         side_sums = {}
         g_tiles = {}
-
         def bias_of(r):
             cc = ROUND_LIST[r][0]
             return bias_all[:, cc * WIDE : (cc + 1) * WIDE]
@@ -233,44 +246,69 @@ def tile_ms_spatial_bottleneck_layer_pa_kernel(tc, sp_prev, spx, gcn_w, gcn_b, A
                 out=out[n, cc * P : (cc + 1) * P, first : first + count].rearrange("c t w -> c (t w)"), in_=result[:]
             )
 
+        spread_bias(0)
+        turn_pair(0, 0)
+        turn_pair(0, 1)
+        spread_bias(1)
+        prepare_adjacency()
+        sum_frame(0)
+        sum_frame(1)
+        interleave_frame(0)
+        interleave_frame(1)
+        add_frame(0, 3, y_psum, "y", nc.scalar.copy)
+        quantise_chunk(0)
+        quantise_frames(0, 0, 2)
+        sum_frame(2)
+        turn_pair(1, 0)
+        turn_pair(1, 1)
+        start_batch_norm()
+        refill(0, 1)
         side_copy(0)
+        interleave_frame(2)
         side_add(0)
-        for t in range(1, FRAMES):
-            refill(0, t)
-        for t in range(1, FRAMES):
-            add_bias(0, t)
+        quantise_frames(0, 2, 2)
+        refill(0, 2)
+        refill(0, 3)
+        add_frame(1, 0, y_psum, "y", nc.scalar.copy)
+        add_frame(1, 1, y_psum, "y", nc.scalar.copy)
+        add_bias(0, 1)
         quantise_chunk(1)
+        refill(1, 1)
         side_copy(1)
-        side_add(1)
-        for t in range(1, FRAMES):
-            refill(1, t)
-        for t in range(FRAMES):
-            add_frame(1, t, y_psum, "y", nc.scalar.copy)
-        bn_turned = turn_psum.tile([P, P], BF16, tag="turn")
-        nc.tensor.transpose(bn_turned[:], bn_rows[:], ident_bf16[:])
-        bn_cols = keep.tile([P, 4, CHUNKS], F32)
-        nc.scalar.copy(out=bn_cols[:], in_=bn_turned[:, 0 : 4 * CHUNKS].rearrange("p (i cc) -> p i cc", i=4))
-        std = keep.tile([P, CHUNKS], F32)
-        nc.scalar.activation(out=std[:], in_=bn_cols[:, 3], func=SQRT, bias=eps[:], scale=1.0)
+        add_bias(0, 2)
+        add_bias(0, 3)
         finish_batch_norm()
+        refill(1, 2)
+        refill(1, 3)
+        add_frame(1, 2, turn_psum, "turn", nc.scalar.copy)
+        add_frame(1, 3, turn_psum, "turn", nc.scalar.copy)
+        side_add(1)
+        turn_pair(2, 0)
+        turn_pair(2, 1)
         add_bias(1, 1)
         add_bias(1, 2)
         second_layer(0, 0, FRAMES)
-        quantise_frames(1, 0, FRAMES)
-        add_bias(1, 3)
+        quantise_frames(1, 0, 2)
+        refill(2, 1)
         side_copy(2)
+        add_bias(1, 3)
+        quantise_frames(1, 2, 2)
+        second_layer(1, 0, FRAMES)
+        refill(2, 2)
+        refill(2, 3)
         side_add(2)
-        for t in range(1, FRAMES):
-            refill(2, t)
         side_copy(3)
-        turn_chunk(2)
         for r in range(2, ROUNDS):
             add_bias(r, 1)
             refill(r + 1, 1)
-            second_layer(r - 1, 0, FRAMES)
+            if r > 2:
+                second_layer(r - 1, 0, FRAMES)
             if r == 2 or r == 4:
                 quantise_chunk(r // 2 + 1)
             side_add(r + 1)
+            if r == 2:
+                turn_pair(3, 0)
+                turn_pair(3, 1)
             add_bias(r, 2)
             refill(r + 1, 2)
             side_copy(r + 2)
@@ -278,6 +316,4 @@ def tile_ms_spatial_bottleneck_layer_pa_kernel(tc, sp_prev, spx, gcn_w, gcn_b, A
                 second_layer(r, 0, FRAMES // 2)
             add_bias(r, 3)
             refill(r + 1, 3)
-            if r == 3:
-                turn_chunk(3)
         second_layer(ROUNDS - 1, FRAMES // 2, FRAMES // 2)

@@ -20,6 +20,7 @@ TOKENS = FRAMES * JOINTS
 WIDE = P * SUBSETS
 ROUND_LIST = [(0, 0), (1, 0), (0, 1), (1, 1), (2, 0), (2, 1), (3, 0), (3, 1)]
 ROUNDS = len(ROUND_LIST)
+SIDE = [1,1,0,1,1,1,1,1]
 BIAS_RUN = SUBSETS * CHANNELS // P
 EPS = 1e-5
 
@@ -66,9 +67,9 @@ def tile_ms_spatial_bottleneck_layer_pa_kernel(tc, sp_prev, spx, gcn_w, gcn_b, A
         w_raw = keep.tile([P, CHUNKS, SUBSETS, CHANNELS], BF16)
         w_rows = gcn_w.rearrange("(k cc p) c -> cc p k c", k=SUBSETS, cc=CHUNKS)
         nc.sync.dma_start(out=w_raw[:, 0], in_=w_rows[0])
+        load_activations(0)
         nc.sync.dma_start(out=a_raw[:], in_=A.rearrange("k v w -> v k w"))
         nc.sync.dma_start(out=pa_raw[:], in_=PA.rearrange("k v w -> v k w"))
-        load_activations(0)
         nc.sync.dma_start(out=w_raw[:, 1], in_=w_rows[1])
         for i, vec in enumerate((bg, bb, bm, bv)):
             nc.sync.dma_start(out=bn_rows[CHUNKS * i : CHUNKS * (i + 1), :], in_=vec.rearrange("(cc p) -> cc p", p=P))
@@ -114,9 +115,13 @@ def tile_ms_spatial_bottleneck_layer_pa_kernel(tc, sp_prev, spx, gcn_w, gcn_b, A
         adj_codes = keep.tile([P, JOINTS], U32, align_bytes=64)
         adj_scales = keep.tile([P, JOINTS], U8, align_bytes=64)
 
-        def prepare_adjacency():
+        def sum_adjacency():
             nc.vector.tensor_tensor(out=adj_sum[:], in0=a_raw[:], in1=pa_raw[:], op=ADD)
-            nc.vector.tensor_copy(out=adj_grouped[:], in_=adj_sum[:].rearrange("v k w -> v w k"))
+
+        def interleave_adjacency():
+            nc.scalar.copy(out=adj_grouped[:], in_=adj_sum[:].rearrange("v k w -> v w k"))
+
+        def quantise_adjacency():
             nc.vector.quantize_mx(
                 out=adj_codes[:].bitcast(FP8X4), scales=adj_scales[:], in_=adj_grouped[:].rearrange("v w k -> v (w k)")
             )
@@ -158,7 +163,7 @@ def tile_ms_spatial_bottleneck_layer_pa_kernel(tc, sp_prev, spx, gcn_w, gcn_b, A
         std = keep.tile([P, CHUNKS], F32)
 
         def start_batch_norm():
-            bn_turned = turn_psum.tile([P, P], BF16, tag="turn")
+            bn_turned = side_psum.tile([P, P], BF16, tag="side")
             nc.tensor.transpose(bn_turned[:], bn_rows[:], ident_bf16[:])
             nc.scalar.copy(out=bn_cols[:], in_=bn_turned[:, 0 : 4 * CHUNKS].rearrange("p (i cc) -> p i cc", i=4))
             nc.scalar.activation(out=std[:], in_=bn_cols[:, 3], func=SQRT, bias=eps[:], scale=1.0)
@@ -198,24 +203,39 @@ def tile_ms_spatial_bottleneck_layer_pa_kernel(tc, sp_prev, spx, gcn_w, gcn_b, A
             if r < ROUNDS:
                 banks[(r, t)] = first_pass(r, t, acc_psum, "acc")
 
+        def own_frames(r):
+            return list(range(SIDE[r], FRAMES)) if r < ROUNDS else []
+
         def side_copy(r):
             if r < ROUNDS:
-                side_bank = first_pass(r, 0, side_psum, "side")
-                side_sum = work.tile([P, WIDE], F32)
-                nc.scalar.copy(out=side_sum[:], in_=side_bank[:])
-                side_sums[r] = side_sum
+                for t in range(SIDE[r]):
+                    side_bank = first_pass(r, t, side_psum, "side")
+                    side_sum = work.tile([P, WIDE], F32)
+                    nc.scalar.copy(out=side_sum[:], in_=side_bank[:])
+                    side_sums[(r, t)] = side_sum
 
         def side_add(r):
             if r < ROUNDS:
                 g_grouped = g_pool.tile([P, FRAMES, WIDE], BF16, align_bytes=64)
-                nc.gpsimd.tensor_tensor(out=g_grouped[:, 0], in0=side_sums[r][:], in1=bias_of(r), op=ADD)
+                for t in range(SIDE[r]):
+                    nc.gpsimd.tensor_tensor(out=g_grouped[:, t], in0=side_sums[(r, t)][:], in1=bias_of(r), op=ADD)
                 g_tiles[r] = g_grouped
+
+        flow = [(r, t) for r in range(ROUNDS) for t in own_frames(r)]
+
+        def fill(i):
+            if i < len(flow):
+                refill(*flow[i])
+
+        def add(i):
+            add_bias(*flow[i])
 
         def add_bias(r, t):
             nc.vector.tensor_tensor(out=g_tiles[r][:, t], in0=banks[(r, t)][:], in1=bias_of(r), op=ADD)
 
-        def second_layer(r, first, count):
-            cc, n = ROUND_LIST[r]
+        g_quantised = {}
+
+        def quantise_g(r, first, count):
             g_codes = work.tile([P, count, P], U32, align_bytes=64)
             g_scales = work.tile([P, count, P], U8, align_bytes=64)
             nc.vector.quantize_mx(
@@ -223,6 +243,11 @@ def tile_ms_spatial_bottleneck_layer_pa_kernel(tc, sp_prev, spx, gcn_w, gcn_b, A
                 scales=g_scales[:].rearrange("v t c -> v (t c)"),
                 in_=g_tiles[r][:, first : first + count].rearrange("v t x -> v (t x)"),
             )
+            g_quantised[(r, first)] = (g_codes, g_scales)
+
+        def multiply_g(r, first, count):
+            cc, n = ROUND_LIST[r]
+            g_codes, g_scales = g_quantised[(r, first)]
             y = y_psum.tile([P, count, JOINTS], F32, tag="y")
             for t in range(count):
                 nc.tensor.matmul_mx(
@@ -246,11 +271,14 @@ def tile_ms_spatial_bottleneck_layer_pa_kernel(tc, sp_prev, spx, gcn_w, gcn_b, A
                 out=out[n, cc * P : (cc + 1) * P, first : first + count].rearrange("c t w -> c (t w)"), in_=result[:]
             )
 
+        def second_layer(r, first, count):
+            quantise_g(r, first, count)
+            multiply_g(r, first, count)
+
         spread_bias(0)
         turn_pair(0, 0)
         turn_pair(0, 1)
         spread_bias(1)
-        prepare_adjacency()
         sum_frame(0)
         sum_frame(1)
         interleave_frame(0)
@@ -259,61 +287,73 @@ def tile_ms_spatial_bottleneck_layer_pa_kernel(tc, sp_prev, spx, gcn_w, gcn_b, A
         quantise_chunk(0)
         quantise_frames(0, 0, 2)
         sum_frame(2)
+        start_batch_norm()
         turn_pair(1, 0)
         turn_pair(1, 1)
-        start_batch_norm()
-        refill(0, 1)
+        fill(0)
         side_copy(0)
         interleave_frame(2)
         side_add(0)
         quantise_frames(0, 2, 2)
-        refill(0, 2)
-        refill(0, 3)
+        fill(1)
+        fill(2)
         add_frame(1, 0, y_psum, "y", nc.scalar.copy)
         add_frame(1, 1, y_psum, "y", nc.scalar.copy)
-        add_bias(0, 1)
+        add(0)
+        sum_adjacency()
         quantise_chunk(1)
-        refill(1, 1)
+        fill(3)
         side_copy(1)
-        add_bias(0, 2)
-        add_bias(0, 3)
-        finish_batch_norm()
-        refill(1, 2)
-        refill(1, 3)
+        interleave_adjacency()
         add_frame(1, 2, turn_psum, "turn", nc.scalar.copy)
+        add(1)
+        fill(4)
         add_frame(1, 3, turn_psum, "turn", nc.scalar.copy)
+        add(2)
+        fill(5)
+        finish_batch_norm()
         side_add(1)
         turn_pair(2, 0)
         turn_pair(2, 1)
-        add_bias(1, 1)
-        add_bias(1, 2)
-        second_layer(0, 0, FRAMES)
+        n0, n1, n2, n3 = len(own_frames(0)), len(own_frames(1)), len(own_frames(2)), len(own_frames(3))
+        base = n0
+        for i in range(3, base):
+            add(i)
+            fill(i + 3)
+        for i in range(base, base + n1):
+            add(i)
+            if i + 3 < base + n1:
+                fill(i + 3)
         quantise_frames(1, 0, 2)
-        refill(2, 1)
-        side_copy(2)
-        add_bias(1, 3)
+        quantise_adjacency()
+        quantise_g(0, 0, FRAMES)
+        fill(6)
+        fill(7)
+        multiply_g(0, 0, FRAMES)
         quantise_frames(1, 2, 2)
-        second_layer(1, 0, FRAMES)
-        refill(2, 2)
-        refill(2, 3)
+        fill(8)
+        quantise_g(1, 0, FRAMES)
+        side_copy(2)
         side_add(2)
         side_copy(3)
+        multiply_g(1, 0, FRAMES)
+        i = base + n1
         for r in range(2, ROUNDS):
-            add_bias(r, 1)
-            refill(r + 1, 1)
-            if r > 2:
-                second_layer(r - 1, 0, FRAMES)
-            if r == 2 or r == 4:
-                quantise_chunk(r // 2 + 1)
-            side_add(r + 1)
-            if r == 2:
-                turn_pair(3, 0)
-                turn_pair(3, 1)
-            add_bias(r, 2)
-            refill(r + 1, 2)
-            side_copy(r + 2)
-            if r == ROUNDS - 1:
-                second_layer(r, 0, FRAMES // 2)
-            add_bias(r, 3)
-            refill(r + 1, 3)
+            for j in range(len(own_frames(r))):
+                add(i)
+                fill(i + 3)
+                i += 1
+                if j == 0:
+                    if r > 2:
+                        second_layer(r - 1, 0, FRAMES)
+                    if r == 2 or r == 4:
+                        quantise_chunk(r // 2 + 1)
+                    side_add(r + 1)
+                    if r == 2:
+                        turn_pair(3, 0)
+                        turn_pair(3, 1)
+                if j == 1:
+                    side_copy(r + 2)
+                if r == ROUNDS - 1 and j == len(own_frames(r)) - 2:
+                    second_layer(r, 0, FRAMES // 2)
         second_layer(ROUNDS - 1, FRAMES // 2, FRAMES // 2)

@@ -58,11 +58,20 @@ def tile_ms_spatial_bottleneck_layer_pa_kernel(tc, sp_prev, spx, gcn_w, gcn_b, A
         pa_raw = keep.tile([P, SUBSETS, JOINTS], BF16)
 
         def load_activations(n):
-            for raw, src in ((prev_raw, sp_prev), (x_raw, spx)):
-                nc.sync.dma_start(
-                    out=raw[:, n].rearrange("q (u e) x -> q u (e x)", u=2),
-                    in_=src[n].rearrange("(u q e) t v -> q u (e t v)", u=2, e=2),
-                )
+            pairs = ((prev_raw, sp_prev), (x_raw, spx))
+            if n == 0:
+                for u in range(2):
+                    for raw, src in pairs:
+                        nc.sync.dma_start(
+                            out=raw[:, n, 2 * u : 2 * u + 2].rearrange("q e x -> q (e x)"),
+                            in_=src[n].rearrange("(u q e) t v -> u q (e t v)", u=2, e=2)[u],
+                        )
+            else:
+                for raw, src in pairs:
+                    nc.sync.dma_start(
+                        out=raw[:, n].rearrange("q (u e) x -> q u (e x)", u=2),
+                        in_=src[n].rearrange("(u q e) t v -> q u (e t v)", u=2, e=2),
+                    )
 
         w_raw = keep.tile([P, CHUNKS, SUBSETS, CHANNELS], BF16)
         w_rows = gcn_w.rearrange("(k cc p) c -> cc p k c", k=SUBSETS, cc=CHUNKS)
@@ -138,9 +147,10 @@ def tile_ms_spatial_bottleneck_layer_pa_kernel(tc, sp_prev, spx, gcn_w, gcn_b, A
             nc.tensor.matmul(total[:], lhsT=ident_bf16[:], rhs=x_raw[:, n, :, joints], start=False, stop=True)
             copy(out=sp_grouped[:, n, joints], in_=total[:].rearrange("q j v -> q v j"))
 
-        def sum_frame(t):
-            joints = slice(t * JOINTS, (t + 1) * JOINTS)
-            nc.vector.tensor_tensor(out=sp_sum[:, :, joints], in0=prev_raw[:, 0, :, joints], in1=x_raw[:, 0, :, joints], op=ADD)
+        def sum_frames(u, first, count):
+            joints = slice(first * JOINTS, (first + count) * JOINTS)
+            pair = slice(2 * u, 2 * u + 2)
+            nc.vector.tensor_tensor(out=sp_sum[:, pair, joints], in0=prev_raw[:, 0, pair, joints], in1=x_raw[:, 0, pair, joints], op=ADD)
 
         def interleave_frame(t):
             joints = slice(t * JOINTS, (t + 1) * JOINTS)
@@ -248,7 +258,8 @@ def tile_ms_spatial_bottleneck_layer_pa_kernel(tc, sp_prev, spx, gcn_w, gcn_b, A
         def multiply_g(r, first, count):
             cc, n = ROUND_LIST[r]
             g_codes, g_scales = g_quantised[(r, first)]
-            y = y_psum.tile([P, count, JOINTS], F32, tag="y")
+            pool, tag = (acc_psum, "acc") if r == ROUNDS - 1 else (y_psum, "y")
+            y = pool.tile([P, count, JOINTS], F32, tag=tag)
             for t in range(count):
                 nc.tensor.matmul_mx(
                     out=y[:, t],
@@ -279,14 +290,14 @@ def tile_ms_spatial_bottleneck_layer_pa_kernel(tc, sp_prev, spx, gcn_w, gcn_b, A
         turn_pair(0, 0)
         turn_pair(0, 1)
         spread_bias(1)
-        sum_frame(0)
-        sum_frame(1)
+        sum_frames(0, 0, 3)
+        sum_frames(1, 0, 2)
         interleave_frame(0)
         interleave_frame(1)
         add_frame(0, 3, y_psum, "y", nc.scalar.copy)
-        quantise_chunk(0)
         quantise_frames(0, 0, 2)
-        sum_frame(2)
+        sum_frames(1, 2, 1)
+        quantise_chunk(0)
         start_batch_norm()
         turn_pair(1, 0)
         turn_pair(1, 1)
@@ -305,12 +316,12 @@ def tile_ms_spatial_bottleneck_layer_pa_kernel(tc, sp_prev, spx, gcn_w, gcn_b, A
         fill(3)
         side_copy(1)
         interleave_adjacency()
-        add_frame(1, 2, turn_psum, "turn", nc.scalar.copy)
         add(1)
         fill(4)
-        add_frame(1, 3, turn_psum, "turn", nc.scalar.copy)
+        add_frame(1, 2, turn_psum, "turn", nc.scalar.copy)
         add(2)
         fill(5)
+        add_frame(1, 3, turn_psum, "turn", nc.scalar.copy)
         finish_batch_norm()
         side_add(1)
         turn_pair(2, 0)
@@ -356,4 +367,7 @@ def tile_ms_spatial_bottleneck_layer_pa_kernel(tc, sp_prev, spx, gcn_w, gcn_b, A
                     side_copy(r + 2)
                 if r == ROUNDS - 1 and j == len(own_frames(r)) - 2:
                     second_layer(r, 0, FRAMES // 2)
-        second_layer(ROUNDS - 1, FRAMES // 2, FRAMES // 2)
+        quantise_g(ROUNDS - 1, 2, 1)
+        quantise_g(ROUNDS - 1, 3, 1)
+        multiply_g(ROUNDS - 1, 2, 1)
+        multiply_g(ROUNDS - 1, 3, 1)

@@ -9,6 +9,7 @@ U32 = mybir.dt.uint32
 U8 = mybir.dt.uint8
 FP8X4 = mybir.dt.float8_e4m3fn_x4
 ADD = mybir.AluOpType.add
+IDENTITY = mybir.ActivationFunctionType.Identity
 RELU = mybir.ActivationFunctionType.Relu
 SQRT = mybir.ActivationFunctionType.Sqrt
 
@@ -20,7 +21,8 @@ TOKENS = FRAMES * JOINTS
 WIDE = P * SUBSETS
 ROUND_LIST = [(0, 0), (1, 0), (0, 1), (1, 1), (2, 0), (2, 1), (3, 0), (3, 1)]
 ROUNDS = len(ROUND_LIST)
-SIDE = [1,1,0,1,1,1,1,1]
+SIDE = [1,1,0,1,1,1,0,0]
+TURNED = [0,0,0,0,1,1,1,1]
 BIAS_RUN = SUBSETS * CHANNELS // P
 EPS = 1e-5
 
@@ -214,7 +216,49 @@ def tile_ms_spatial_bottleneck_layer_pa_kernel(tc, sp_prev, spx, gcn_w, gcn_b, A
                 banks[(r, t)] = first_pass(r, t, acc_psum, "acc")
 
         def own_frames(r):
-            return list(range(SIDE[r], FRAMES)) if r < ROUNDS else []
+            return list(range(SIDE[r] + TURNED[r], FRAMES)) if r < ROUNDS else []
+
+        bias_cols = keep.tile([P, 2 * SUBSETS], F32)
+
+        def turn_bias():
+            turned = y_psum.tile([P, 2 * SUBSETS, P], BF16, tag="y")
+            for b in range(2 * SUBSETS):
+                first = 2 * WIDE + b * P
+                nc.tensor.transpose(turned[:, b, :], bias_all[:, first : first + P], ident_bf16[:])
+            nc.scalar.copy(out=bias_cols[:], in_=turned[:, :, 0])
+
+        turned_sums = {}
+
+        def turned_pass(r):
+            if r < ROUNDS and TURNED[r]:
+                t = SIDE[r]
+                cc, n = ROUND_LIST[r]
+                joints = slice(t * JOINTS, (t + 1) * JOINTS)
+                bank = turn_psum.tile([P, SUBSETS, JOINTS], F32, tag="turn")
+                sums = work.tile([P, SUBSETS, JOINTS], BF16)
+                for b in range(SUBSETS):
+                    cols = slice(b * P, (b + 1) * P)
+                    nc.tensor.matmul_mx(
+                        out=bank[:, b],
+                        lhsT=w_codes[:, cc, cols].bitcast(FP8X4),
+                        lhsT_scale=w_scales[:, cc, cols],
+                        rhs=sp_codes[:, n, joints].bitcast(FP8X4),
+                        rhs_scale=sp_scales[:, n, joints],
+                        start=True,
+                        stop=True,
+                    )
+                for b in range(SUBSETS):
+                    c = SUBSETS * (cc - 2) + b
+                    nc.scalar.activation(out=sums[:, b], in_=bank[:, b], func=IDENTITY, bias=bias_cols[:, c : c + 1], scale=1.0)
+                turned_sums[r] = sums
+
+        def turned_back(r):
+            if r < ROUNDS and TURNED[r]:
+                t = SIDE[r]
+                back = turn_psum.tile([P, SUBSETS, P], BF16, tag="turn")
+                for b in range(SUBSETS):
+                    nc.tensor.transpose(back[:, b, :], turned_sums[r][:, b], ident_bf16[:])
+                nc.scalar.copy(out=g_tiles[r][:, t], in_=back[:].rearrange("v b o -> v (b o)"))
 
         def side_copy(r):
             if r < ROUNDS:
@@ -322,6 +366,7 @@ def tile_ms_spatial_bottleneck_layer_pa_kernel(tc, sp_prev, spx, gcn_w, gcn_b, A
         add(2)
         fill(5)
         add_frame(1, 3, turn_psum, "turn", nc.scalar.copy)
+        turn_bias()
         finish_batch_norm()
         side_add(1)
         turn_pair(2, 0)
@@ -356,15 +401,21 @@ def tile_ms_spatial_bottleneck_layer_pa_kernel(tc, sp_prev, spx, gcn_w, gcn_b, A
                 i += 1
                 if j == 0:
                     if r > 2:
-                        second_layer(r - 1, 0, FRAMES)
+                        quantise_g(r - 1, 0, FRAMES)
                     if r == 2 or r == 4:
                         quantise_chunk(r // 2 + 1)
                     side_add(r + 1)
                     if r == 2:
                         turn_pair(3, 0)
                         turn_pair(3, 1)
+                    if r > 2:
+                        side_copy(r + 2)
+                        multiply_g(r - 1, 0, FRAMES)
+                    turned_back(r + 1)
                 if j == 1:
-                    side_copy(r + 2)
+                    if r == 2:
+                        side_copy(r + 2)
+                    turned_pass(r + 2)
                 if r == ROUNDS - 1 and j == len(own_frames(r)) - 2:
                     second_layer(r, 0, FRAMES // 2)
         quantise_g(ROUNDS - 1, 2, 1)

@@ -22,7 +22,7 @@ WIDE = P * SUBSETS
 ROUND_LIST = [(0, 0), (1, 0), (0, 1), (1, 1), (2, 0), (2, 1), (3, 0), (3, 1)]
 ROUNDS = len(ROUND_LIST)
 SIDE = [1,1,0,1,1,1,0,0]
-TURNED = [0,0,0,0,1,1,1,1]
+TURNED = [0,0,0,0,1,1,2,1]
 BIAS_RUN = SUBSETS * CHANNELS // P
 EPS = 1e-5
 
@@ -34,6 +34,7 @@ def tile_ms_spatial_bottleneck_layer_pa_kernel(tc, sp_prev, spx, gcn_w, gcn_b, A
     with ExitStack() as stack:
         keep = stack.enter_context(tc.tile_pool(name="keep", bufs=1))
         work = stack.enter_context(tc.tile_pool(name="work", bufs=4))
+        out_pool = stack.enter_context(tc.tile_pool(name="out_pool", bufs=ROUNDS + 2))
         g_pool = stack.enter_context(tc.tile_pool(name="g_pool", bufs=2))
         acc_psum = stack.enter_context(tc.psum_pool(name="acc_psum", bufs=FRAMES - 1))
         side_psum = stack.enter_context(tc.psum_pool(name="side_psum", bufs=1))
@@ -229,9 +230,11 @@ def tile_ms_spatial_bottleneck_layer_pa_kernel(tc, sp_prev, spx, gcn_w, gcn_b, A
 
         turned_sums = {}
 
-        def turned_pass(r):
-            if r < ROUNDS and TURNED[r]:
-                t = SIDE[r]
+        def turned_frames(r):
+            return range(SIDE[r], SIDE[r] + TURNED[r]) if r < ROUNDS else ()
+
+        def turned_pass(r, k=0):
+            for t in turned_frames(r)[k : k + 1]:
                 cc, n = ROUND_LIST[r]
                 joints = slice(t * JOINTS, (t + 1) * JOINTS)
                 bank = turn_psum.tile([P, SUBSETS, JOINTS], F32, tag="turn")
@@ -250,14 +253,13 @@ def tile_ms_spatial_bottleneck_layer_pa_kernel(tc, sp_prev, spx, gcn_w, gcn_b, A
                 for b in range(SUBSETS):
                     c = SUBSETS * (cc - 2) + b
                     nc.scalar.activation(out=sums[:, b], in_=bank[:, b], func=IDENTITY, bias=bias_cols[:, c : c + 1], scale=1.0)
-                turned_sums[r] = sums
+                turned_sums[(r, t)] = sums
 
-        def turned_back(r):
-            if r < ROUNDS and TURNED[r]:
-                t = SIDE[r]
+        def turned_back(r, k=0):
+            for t in turned_frames(r)[k : k + 1]:
                 back = turn_psum.tile([P, SUBSETS, P], BF16, tag="turn")
                 for b in range(SUBSETS):
-                    nc.tensor.transpose(back[:, b, :], turned_sums[r][:, b], ident_bf16[:])
+                    nc.tensor.transpose(back[:, b, :], turned_sums[(r, t)][:, b], ident_bf16[:])
                 nc.scalar.copy(out=g_tiles[r][:, t], in_=back[:].rearrange("v b o -> v (b o)"))
 
         def side_copy(r):
@@ -314,7 +316,7 @@ def tile_ms_spatial_bottleneck_layer_pa_kernel(tc, sp_prev, spx, gcn_w, gcn_b, A
                     start=True,
                     stop=True,
                 )
-            result = work.tile([P, count * JOINTS], F32)
+            result = out_pool.tile([P, count * JOINTS], F32)
             nc.scalar.activation(
                 out=result[:],
                 in_=y[:].rearrange("c t w -> c (t w)"),
@@ -371,29 +373,26 @@ def tile_ms_spatial_bottleneck_layer_pa_kernel(tc, sp_prev, spx, gcn_w, gcn_b, A
         side_add(1)
         turn_pair(2, 0)
         turn_pair(2, 1)
-        n0, n1, n2, n3 = len(own_frames(0)), len(own_frames(1)), len(own_frames(2)), len(own_frames(3))
-        base = n0
-        for i in range(3, base):
+        first = len(own_frames(0))
+        last = first + len(own_frames(1))
+        for i in range(first, last):
             add(i)
-            fill(i + 3)
-        for i in range(base, base + n1):
-            add(i)
-            if i + 3 < base + n1:
+            if i + 3 < last:
                 fill(i + 3)
         quantise_frames(1, 0, 2)
         quantise_adjacency()
         quantise_g(0, 0, FRAMES)
-        fill(6)
-        fill(7)
+        fill(last)
+        fill(last + 1)
         multiply_g(0, 0, FRAMES)
         quantise_frames(1, 2, 2)
-        fill(8)
+        fill(last + 2)
         quantise_g(1, 0, FRAMES)
         side_copy(2)
         side_add(2)
         side_copy(3)
         multiply_g(1, 0, FRAMES)
-        i = base + n1
+        i = last
         for r in range(2, ROUNDS):
             for j in range(len(own_frames(r))):
                 add(i)
@@ -412,13 +411,15 @@ def tile_ms_spatial_bottleneck_layer_pa_kernel(tc, sp_prev, spx, gcn_w, gcn_b, A
                         side_copy(r + 2)
                         multiply_g(r - 1, 0, FRAMES)
                     turned_back(r + 1)
+                    turned_back(r + 1, 1)
                 if j == 1:
                     if r == 2:
                         side_copy(r + 2)
                     turned_pass(r + 2)
-                if r == ROUNDS - 1 and j == len(own_frames(r)) - 2:
-                    second_layer(r, 0, FRAMES // 2)
-        quantise_g(ROUNDS - 1, 2, 1)
+                    turned_pass(r + 2, 1)
+                if r == ROUNDS - 1 and j == 1:
+                    second_layer(r, 1, 2)
+        quantise_g(ROUNDS - 1, 0, 1)
         quantise_g(ROUNDS - 1, 3, 1)
-        multiply_g(ROUNDS - 1, 2, 1)
+        multiply_g(ROUNDS - 1, 0, 1)
         multiply_g(ROUNDS - 1, 3, 1)

from contextlib import ExitStack

import concourse.mybir as mybir
from concourse.masks import make_identity

BF16 = mybir.dt.bfloat16
F32 = mybir.dt.float32
U32 = mybir.dt.uint32
U8 = mybir.dt.uint8
FP8X4 = mybir.dt.float8_e4m3fn_x4
ADD = mybir.AluOpType.add
IDENTITY = mybir.ActivationFunctionType.Identity
RELU = mybir.ActivationFunctionType.Relu
SQRT = mybir.ActivationFunctionType.Sqrt

P = 128
PACK = 4
BATCH, FRAMES, JOINTS, SUBSETS, CHANNELS = 2, 4, 128, 4, 512
CHUNKS = CHANNELS // P
TOKENS = FRAMES * JOINTS
WIDE = P * SUBSETS
ROUND_LIST = [(0, 0), (1, 0), (0, 1), (1, 1), (2, 0), (2, 1), (3, 0), (3, 1)]
ROUNDS = len(ROUND_LIST)
SIDE = [1,1,0,1,1,1,0,0]
TURNED = [0,0,0,0,1,1,2,1]
BIAS_RUN = SUBSETS * CHANNELS // P
EPS = 1e-5

FLOPS = 2 * BATCH * TOKENS * SUBSETS * CHANNELS * CHANNELS + 2 * BATCH * FRAMES * CHANNELS * SUBSETS * JOINTS * JOINTS


def tile_ms_spatial_bottleneck_layer_pa_kernel(tc, sp_prev, spx, gcn_w, gcn_b, A, PA, bg, bb, bm, bv, out):
    nc = tc.nc
    with ExitStack() as stack:
        keep = stack.enter_context(tc.tile_pool(name="keep", bufs=1))
        work = stack.enter_context(tc.tile_pool(name="work", bufs=4))
        out_pool = stack.enter_context(tc.tile_pool(name="out_pool", bufs=ROUNDS + 2))
        g_pool = stack.enter_context(tc.tile_pool(name="g_pool", bufs=2))
        acc_psum = stack.enter_context(tc.psum_pool(name="acc_psum", bufs=FRAMES - 1))
        side_psum = stack.enter_context(tc.psum_pool(name="side_psum", bufs=1))
        turn_psum = stack.enter_context(tc.psum_pool(name="turn_psum", bufs=2))
        y_psum = stack.enter_context(tc.psum_pool(name="y_psum", bufs=2))

        stack.enter_context(tc.manual_schedule())
        ident_bf16 = keep.tile([P, P], BF16)
        make_identity(nc, ident_bf16[:])
        ident_f32 = keep.tile([P, P], F32)
        make_identity(nc, ident_f32[:])
        bn_rows = keep.tile([P, P], BF16)
        nc.vector.memset(bn_rows[:], 0.0)
        eps = keep.tile([P, 1], F32)
        nc.vector.memset(eps[:], EPS)
        warm = keep.tile([P, 1], F32)
        nc.scalar.sqrt(out=warm[:], in_=eps[:])

        bias_runs = keep.tile([P, BIAS_RUN], BF16)
        nc.sync.dma_start(out=bias_runs[:], in_=gcn_b.rearrange("(p m) -> p m", m=BIAS_RUN))
        prev_raw = keep.tile([P, BATCH, PACK, TOKENS], BF16)
        x_raw = keep.tile([P, BATCH, PACK, TOKENS], BF16)
        a_raw = keep.tile([P, SUBSETS, JOINTS], BF16)
        pa_raw = keep.tile([P, SUBSETS, JOINTS], BF16)

        def load_activations(n):
            pairs = ((prev_raw, sp_prev), (x_raw, spx))
            if n == 0:
                for u in range(2):
                    for raw, src in pairs:
                        nc.sync.dma_start(
                            out=raw[:, n, 2 * u : 2 * u + 2].rearrange("q e x -> q (e x)"),
                            in_=src[n].rearrange("(u q e) t v -> u q (e t v)", u=2, e=2)[u],
                        )
            else:
                for raw, src in pairs:
                    nc.sync.dma_start(
                        out=raw[:, n].rearrange("q (u e) x -> q u (e x)", u=2),
                        in_=src[n].rearrange("(u q e) t v -> q u (e t v)", u=2, e=2),
                    )

        w_raw = keep.tile([P, CHUNKS, SUBSETS, CHANNELS], BF16)
        w_rows = gcn_w.rearrange("(k cc p) c -> cc p k c", k=SUBSETS, cc=CHUNKS)
        nc.sync.dma_start(out=w_raw[:, 0], in_=w_rows[0])
        load_activations(0)
        nc.sync.dma_start(out=a_raw[:], in_=A.rearrange("k v w -> v k w"))
        nc.sync.dma_start(out=pa_raw[:], in_=PA.rearrange("k v w -> v k w"))
        nc.sync.dma_start(out=w_raw[:, 1], in_=w_rows[1])
        for i, vec in enumerate((bg, bb, bm, bv)):
            nc.sync.dma_start(out=bn_rows[CHUNKS * i : CHUNKS * (i + 1), :], in_=vec.rearrange("(cc p) -> cc p", p=P))
        load_activations(1)
        for cc in range(2, CHUNKS):
            nc.sync.dma_start(out=w_raw[:, cc], in_=w_rows[cc])

        w_grouped = keep.tile([P, CHUNKS, WIDE * PACK], BF16, align_bytes=64)
        w_codes = keep.tile([P, CHUNKS, WIDE], U32, align_bytes=64)
        w_scales = keep.tile([P, CHUNKS, WIDE], U8, align_bytes=64)
        bias_all = keep.tile([P, CHUNKS * WIDE], BF16)

        def turn_pair(cc, pair):
            words_out = w_grouped[:, cc].bitcast(F32).rearrange("q (c k u) -> q c k u", k=SUBSETS, u=2)
            turned = turn_psum.tile([P, 2, 2, P], F32, tag="turn")
            for k2 in range(2):
                for u in range(2):
                    nc.tensor.transpose(
                        turned[:, k2, u, :], w_raw[:, cc, 2 * pair + k2, :].bitcast(F32)[:, u * P : (u + 1) * P], ident_f32[:]
                    )
            nc.scalar.copy(out=words_out[:, :, 2 * pair : 2 * pair + 2, :], in_=turned[:].rearrange("q k u c -> q c k u"))

        def quantise_chunk(cc):
            nc.vector.quantize_mx(out=w_codes[:, cc].bitcast(FP8X4), scales=w_scales[:, cc], in_=w_grouped[:, cc])

        per_bank = BIAS_RUN // 2
        bias_out = bias_all[:].rearrange("p (x m k) -> p x m k", m=BIAS_RUN, k=SUBSETS)

        def spread_bias(half):
            spread = turn_psum.tile([P, per_bank, P], BF16, tag="turn")
            for m in range(per_bank):
                first = half * per_bank + m
                nc.tensor.matmul(
                    spread[:, m, :], lhsT=bias_runs[:, first : first + 1].to_broadcast([P, P]), rhs=ident_bf16[:], start=True, stop=True
                )
            nc.scalar.copy(
                out=bias_out[:, :, half * per_bank : (half + 1) * per_bank, :],
                in_=spread[:].rearrange("p m (k x) -> p x m k", k=SUBSETS),
            )

        adj_sum = keep.tile([P, SUBSETS, JOINTS], BF16)
        adj_grouped = keep.tile([P, JOINTS, SUBSETS], BF16, align_bytes=64)
        adj_codes = keep.tile([P, JOINTS], U32, align_bytes=64)
        adj_scales = keep.tile([P, JOINTS], U8, align_bytes=64)

        def sum_adjacency():
            nc.vector.tensor_tensor(out=adj_sum[:], in0=a_raw[:], in1=pa_raw[:], op=ADD)

        def interleave_adjacency():
            nc.scalar.copy(out=adj_grouped[:], in_=adj_sum[:].rearrange("v k w -> v w k"))

        def quantise_adjacency():
            nc.vector.quantize_mx(
                out=adj_codes[:].bitcast(FP8X4), scales=adj_scales[:], in_=adj_grouped[:].rearrange("v w k -> v (w k)")
            )

        sp_sum = keep.tile([P, PACK, TOKENS], BF16)
        sp_grouped = keep.tile([P, BATCH, TOKENS, PACK], BF16, align_bytes=64)
        sp_codes = keep.tile([P, BATCH, TOKENS], U32, align_bytes=64)
        sp_scales = keep.tile([P, BATCH, TOKENS], U8, align_bytes=64)

        def add_frame(n, t, pool, tag, copy):
            joints = slice(t * JOINTS, (t + 1) * JOINTS)
            total = pool.tile([P, PACK, JOINTS], F32, tag=tag)
            nc.tensor.matmul(total[:], lhsT=ident_bf16[:], rhs=prev_raw[:, n, :, joints], start=True, stop=False)
            nc.tensor.matmul(total[:], lhsT=ident_bf16[:], rhs=x_raw[:, n, :, joints], start=False, stop=True)
            copy(out=sp_grouped[:, n, joints], in_=total[:].rearrange("q j v -> q v j"))

        def sum_frames(u, first, count):
            joints = slice(first * JOINTS, (first + count) * JOINTS)
            pair = slice(2 * u, 2 * u + 2)
            nc.vector.tensor_tensor(out=sp_sum[:, pair, joints], in0=prev_raw[:, 0, pair, joints], in1=x_raw[:, 0, pair, joints], op=ADD)

        def interleave_frame(t):
            joints = slice(t * JOINTS, (t + 1) * JOINTS)
            nc.vector.tensor_copy(
                out=sp_grouped[:, 0, joints].rearrange("q (x i) j -> q x j i", i=4),
                in_=sp_sum[:, :, joints].rearrange("q j (x i) -> q x j i", i=4),
            )

        def quantise_frames(n, first, count):
            joints = slice(first * JOINTS, (first + count) * JOINTS)
            nc.vector.quantize_mx(
                out=sp_codes[:, n, joints].bitcast(FP8X4),
                scales=sp_scales[:, n, joints],
                in_=sp_grouped[:, n, joints].rearrange("q x j -> q (x j)"),
            )

        bn_scale = keep.tile([P, CHUNKS], F32)
        bn_shift = keep.tile([P, CHUNKS], F32)
        bn_cols = keep.tile([P, 4, CHUNKS], F32)
        std = keep.tile([P, CHUNKS], F32)

        def start_batch_norm():
            bn_turned = side_psum.tile([P, P], BF16, tag="side")
            nc.tensor.transpose(bn_turned[:], bn_rows[:], ident_bf16[:])
            nc.scalar.copy(out=bn_cols[:], in_=bn_turned[:, 0 : 4 * CHUNKS].rearrange("p (i cc) -> p i cc", i=4))
            nc.scalar.activation(out=std[:], in_=bn_cols[:, 3], func=SQRT, bias=eps[:], scale=1.0)

        inv_std = keep.tile([P, CHUNKS], F32)
        mean_scaled = keep.tile([P, CHUNKS], F32)

        def finish_batch_norm():
            nc.vector.reciprocal(out=inv_std[:], in_=std[:])
            nc.gpsimd.tensor_mul(out=bn_scale[:], in0=bn_cols[:, 0], in1=inv_std[:])
            nc.gpsimd.tensor_mul(out=mean_scaled[:], in0=bn_cols[:, 2], in1=bn_scale[:])
            nc.gpsimd.tensor_sub(out=bn_shift[:], in0=bn_cols[:, 1], in1=mean_scaled[:])

        banks = {}
        side_sums = {}
        g_tiles = {}
        def bias_of(r):
            cc = ROUND_LIST[r][0]
            return bias_all[:, cc * WIDE : (cc + 1) * WIDE]

        def first_pass(r, t, pool, tag):
            cc, n = ROUND_LIST[r]
            joints = slice(t * JOINTS, (t + 1) * JOINTS)
            acc = pool.tile([P, WIDE], F32, tag=tag)
            nc.tensor.matmul_mx(
                out=acc[:],
                lhsT=sp_codes[:, n, joints].bitcast(FP8X4),
                lhsT_scale=sp_scales[:, n, joints],
                rhs=w_codes[:, cc].bitcast(FP8X4),
                rhs_scale=w_scales[:, cc],
                start=True,
                stop=True,
            )
            return acc

        def refill(r, t):
            if r < ROUNDS:
                banks[(r, t)] = first_pass(r, t, acc_psum, "acc")

        def own_frames(r):
            return list(range(SIDE[r] + TURNED[r], FRAMES)) if r < ROUNDS else []

        bias_cols = keep.tile([P, 2 * SUBSETS], F32)

        def turn_bias():
            turned = y_psum.tile([P, 2 * SUBSETS, P], BF16, tag="y")
            for b in range(2 * SUBSETS):
                first = 2 * WIDE + b * P
                nc.tensor.transpose(turned[:, b, :], bias_all[:, first : first + P], ident_bf16[:])
            nc.scalar.copy(out=bias_cols[:], in_=turned[:, :, 0])

        turned_sums = {}

        def turned_frames(r):
            return range(SIDE[r], SIDE[r] + TURNED[r]) if r < ROUNDS else ()

        def turned_pass(r, k=0):
            for t in turned_frames(r)[k : k + 1]:
                cc, n = ROUND_LIST[r]
                joints = slice(t * JOINTS, (t + 1) * JOINTS)
                bank = turn_psum.tile([P, SUBSETS, JOINTS], F32, tag="turn")
                sums = work.tile([P, SUBSETS, JOINTS], BF16)
                for b in range(SUBSETS):
                    cols = slice(b * P, (b + 1) * P)
                    nc.tensor.matmul_mx(
                        out=bank[:, b],
                        lhsT=w_codes[:, cc, cols].bitcast(FP8X4),
                        lhsT_scale=w_scales[:, cc, cols],
                        rhs=sp_codes[:, n, joints].bitcast(FP8X4),
                        rhs_scale=sp_scales[:, n, joints],
                        start=True,
                        stop=True,
                    )
                for b in range(SUBSETS):
                    c = SUBSETS * (cc - 2) + b
                    nc.scalar.activation(out=sums[:, b], in_=bank[:, b], func=IDENTITY, bias=bias_cols[:, c : c + 1], scale=1.0)
                turned_sums[(r, t)] = sums

        def turned_back(r, k=0):
            for t in turned_frames(r)[k : k + 1]:
                back = turn_psum.tile([P, SUBSETS, P], BF16, tag="turn")
                for b in range(SUBSETS):
                    nc.tensor.transpose(back[:, b, :], turned_sums[(r, t)][:, b], ident_bf16[:])
                nc.scalar.copy(out=g_tiles[r][:, t], in_=back[:].rearrange("v b o -> v (b o)"))

        def side_copy(r):
            if r < ROUNDS:
                for t in range(SIDE[r]):
                    side_bank = first_pass(r, t, side_psum, "side")
                    side_sum = work.tile([P, WIDE], F32)
                    nc.scalar.copy(out=side_sum[:], in_=side_bank[:])
                    side_sums[(r, t)] = side_sum

        def side_add(r):
            if r < ROUNDS:
                g_grouped = g_pool.tile([P, FRAMES, WIDE], BF16, align_bytes=64)
                for t in range(SIDE[r]):
                    nc.gpsimd.tensor_tensor(out=g_grouped[:, t], in0=side_sums[(r, t)][:], in1=bias_of(r), op=ADD)
                g_tiles[r] = g_grouped

        flow = [(r, t) for r in range(ROUNDS) for t in own_frames(r)]

        def fill(i):
            if i < len(flow):
                refill(*flow[i])

        def add(i):
            add_bias(*flow[i])

        def add_bias(r, t):
            nc.vector.tensor_tensor(out=g_tiles[r][:, t], in0=banks[(r, t)][:], in1=bias_of(r), op=ADD)

        g_quantised = {}

        def quantise_g(r, first, count):
            g_codes = work.tile([P, count, P], U32, align_bytes=64)
            g_scales = work.tile([P, count, P], U8, align_bytes=64)
            nc.vector.quantize_mx(
                out=g_codes[:].rearrange("v t c -> v (t c)").bitcast(FP8X4),
                scales=g_scales[:].rearrange("v t c -> v (t c)"),
                in_=g_tiles[r][:, first : first + count].rearrange("v t x -> v (t x)"),
            )
            g_quantised[(r, first)] = (g_codes, g_scales)

        def multiply_g(r, first, count):
            cc, n = ROUND_LIST[r]
            g_codes, g_scales = g_quantised[(r, first)]
            pool, tag = (acc_psum, "acc") if r == ROUNDS - 1 else (y_psum, "y")
            y = pool.tile([P, count, JOINTS], F32, tag=tag)
            for t in range(count):
                nc.tensor.matmul_mx(
                    out=y[:, t],
                    lhsT=g_codes[:, t].bitcast(FP8X4),
                    lhsT_scale=g_scales[:, t],
                    rhs=adj_codes[:].bitcast(FP8X4),
                    rhs_scale=adj_scales[:],
                    start=True,
                    stop=True,
                )
            result = out_pool.tile([P, count * JOINTS], F32)
            nc.scalar.activation(
                out=result[:],
                in_=y[:].rearrange("c t w -> c (t w)"),
                func=RELU,
                bias=bn_shift[:, cc : cc + 1],
                scale=bn_scale[:, cc : cc + 1],
            )
            nc.sync.dma_start(
                out=out[n, cc * P : (cc + 1) * P, first : first + count].rearrange("c t w -> c (t w)"), in_=result[:]
            )

        def second_layer(r, first, count):
            quantise_g(r, first, count)
            multiply_g(r, first, count)

        spread_bias(0)
        turn_pair(0, 0)
        turn_pair(0, 1)
        spread_bias(1)
        sum_frames(0, 0, 3)
        sum_frames(1, 0, 2)
        interleave_frame(0)
        interleave_frame(1)
        add_frame(0, 3, y_psum, "y", nc.scalar.copy)
        quantise_frames(0, 0, 2)
        sum_frames(1, 2, 1)
        quantise_chunk(0)
        start_batch_norm()
        turn_pair(1, 0)
        turn_pair(1, 1)
        fill(0)
        side_copy(0)
        interleave_frame(2)
        side_add(0)
        quantise_frames(0, 2, 2)
        fill(1)
        fill(2)
        add_frame(1, 0, y_psum, "y", nc.scalar.copy)
        add_frame(1, 1, y_psum, "y", nc.scalar.copy)
        add(0)
        sum_adjacency()
        quantise_chunk(1)
        fill(3)
        side_copy(1)
        interleave_adjacency()
        add(1)
        fill(4)
        add_frame(1, 2, turn_psum, "turn", nc.scalar.copy)
        add(2)
        fill(5)
        add_frame(1, 3, turn_psum, "turn", nc.scalar.copy)
        turn_bias()
        finish_batch_norm()
        side_add(1)
        turn_pair(2, 0)
        turn_pair(2, 1)
        first = len(own_frames(0))
        last = first + len(own_frames(1))
        for i in range(first, last):
            add(i)
            if i + 3 < last:
                fill(i + 3)
        quantise_frames(1, 0, 2)
        quantise_adjacency()
        quantise_g(0, 0, FRAMES)
        fill(last)
        fill(last + 1)
        multiply_g(0, 0, FRAMES)
        quantise_frames(1, 2, 2)
        fill(last + 2)
        quantise_g(1, 0, FRAMES)
        side_copy(2)
        side_add(2)
        side_copy(3)
        multiply_g(1, 0, FRAMES)
        i = last
        for r in range(2, ROUNDS):
            for j in range(len(own_frames(r))):
                add(i)
                fill(i + 3)
                i += 1
                if j == 0:
                    if r > 2:
                        quantise_g(r - 1, 0, FRAMES)
                    if r == 2 or r == 4:
                        quantise_chunk(r // 2 + 1)
                    side_add(r + 1)
                    if r == 2:
                        turn_pair(3, 0)
                        turn_pair(3, 1)
                    if r > 2:
                        side_copy(r + 2)
                        multiply_g(r - 1, 0, FRAMES)
                    turned_back(r + 1)
                    turned_back(r + 1, 1)
                if j == 1:
                    if r == 2:
                        side_copy(r + 2)
                    turned_pass(r + 2)
                    turned_pass(r + 2, 1)
                if r == ROUNDS - 1 and j == 1:
                    second_layer(r, 1, 2)
        quantise_g(ROUNDS - 1, 0, 1)
        quantise_g(ROUNDS - 1, 3, 1)
        multiply_g(ROUNDS - 1, 0, 1)
        multiply_g(ROUNDS - 1, 3, 1)
